import numpy as np
import ml_dtypes


def mxq(x, axis, fmt="e4m3"):
    dtype, down = {"e4m3": (ml_dtypes.float8_e4m3fn, 7), "e5m2": (ml_dtypes.float8_e5m2, 14)}[fmt]
    v = np.moveaxis(np.asarray(x, np.float32).astype(ml_dtypes.bfloat16).astype(np.float64), axis, -1)
    blocks = v.reshape(v.shape[:-1] + (-1, 32))
    amax = np.abs(blocks).max(-1, keepdims=True)
    byte = np.maximum(np.where(amax > 0, np.frexp(amax)[1] - 1 + 127, 0) - down, 1)
    scale = np.exp2(byte - 127.0)
    codes = (blocks / scale).astype(np.float32).astype(dtype).astype(np.float64)
    return np.moveaxis((codes * scale).reshape(v.shape), -1, axis)


WIDE = False


def mx_kscale(k):
    if not WIDE:
        return np.ones(k)
    levels = np.array([10, -10, 5, -5, 0])
    if k % 512:
        return np.exp2(np.random.permutation(np.resize(levels, k // 32))).repeat(32)
    a = np.empty((k // 512, 16))
    for p in range(k // 512):
        a[p, :8] = np.random.permutation(np.resize(levels, 8))
        for g in range(8):
            far = levels[np.abs(levels - a[p, g]) >= 10]
            a[p, g + 8] = far[np.random.randint(len(far))]
    return np.exp2(a.ravel()).repeat(32)


BF16 = ml_dtypes.bfloat16


def bf(x):
    return np.asarray(x, np.float32).astype(BF16)


def f64(x):
    return np.asarray(x).astype(np.float64)


B, N, DIM, H, KD, D = 32, 256, 256, 4, 64, 128
DH = H * D
EPS = 1e-5


def hard_swish(v):
    return v * (np.minimum(np.maximum(v + 3.0, 0.0), 6.0) / 6.0)


def setup_inputs():
    t = mx_kscale(DH)
    c = 2.0 ** (-8.0 * np.random.random(DIM))
    return {"h_attn": bf(1.5 * np.random.standard_normal((B, N, DH)) * t),
            "proj_w": bf(np.random.standard_normal((DIM, DH)) * c[:, None] / np.sqrt(DH) / t),
            "proj_g": bf(1.0 + 0.1 * np.random.standard_normal(DIM)),
            "proj_b": bf(0.1 * np.random.standard_normal(DIM))}


def bn(y, g, b):
    m = y.mean(axis=(0, 1))
    v = ((y - m) ** 2).mean(axis=(0, 1))
    return (y - m) * (g / np.sqrt(v + EPS)) + b


def reference(h_attn, proj_w, proj_g, proj_b):
    h = hard_swish(f64(h_attn))
    y = mxq(h, 2, "e4m3") @ mxq(f64(proj_w), 1, "e4m3").T
    return bn(y, f64(proj_g), f64(proj_b))

@@ -1,0 +1,288 @@
+import concourse.mybir as mybir
+from concourse.masks import make_identity
+
+FP8X4 = mybir.dt.float8_e4m3fn_x4
+BF16 = mybir.dt.bfloat16
+F32 = mybir.dt.float32
+U32 = mybir.dt.uint32
+U8 = mybir.dt.uint8
+ACT = mybir.ActivationFunctionType
+ALU = mybir.AluOpType
+X_AXIS = mybir.AxisListType.X
+
+P = 128
+PACK = 4
+K = P * PACK
+ROWS = 32 * 256
+FEATURES = 256
+HALVES = FEATURES // P
+CHUNK = 512
+CHUNKS = ROWS // CHUNK
+BLOCKS = CHUNK // P
+PAIR = 2
+EPS = 1e-5
+
+FLOPS = 2 * ROWS * K * FEATURES
+
+
+def tile_attention_pb_t_kernel(tc, h_attn, proj_w, proj_g, proj_b, out):
+    nc = tc.nc
+
+    x_chunks = h_attn.flatten_outer_dims().rearrange("(i p j) k -> i p j k", p=P, j=BLOCKS)
+    out_chunks = out.flatten_outer_dims().rearrange("(i p j) c -> i p j c", p=P, j=BLOCKS)
+
+    with tc.manual_schedule(), tc.tile_pool(name="keep", bufs=1) as keep, tc.tile_pool(
+        name="loads", bufs=CHUNKS
+    ) as loads, tc.tile_pool(name="stage", bufs=3) as stage:
+        w_rows = keep.tile([P, HALVES, K], BF16)
+        nc.sync.dma_start(out=w_rows[:], in_=proj_w.rearrange("(h c) k -> c h k", h=HALVES))
+        gb_rows = keep.tile([P, P], BF16)
+        nc.vector.memset(gb_rows[:], 0.0)
+        nc.sync.dma_start(
+            out=gb_rows[0:HALVES, :], in_=proj_g.rearrange("(h c) -> h c", h=HALVES)
+        )
+        nc.sync.dma_start(
+            out=gb_rows[HALVES : 2 * HALVES, :], in_=proj_b.rearrange("(h c) -> h c", h=HALVES)
+        )
+        x_tiles = []
+        for chunk in range(CHUNKS):
+            x_rows = loads.tile([P, BLOCKS, K], BF16, name="x_rows")
+            nc.sync.dma_start(out=x_rows[:], in_=x_chunks[chunk])
+            x_tiles.append(x_rows)
+
+        ident_bf16 = keep.tile([P, P], BF16)
+        make_identity(nc, ident_bf16[:])
+        ident_f32 = keep.tile([P, P], F32)
+        make_identity(nc, ident_f32[:])
+
+        one = keep.tile([P, 1], F32)
+        nc.vector.memset(one[:], 1.0)
+        nc.scalar.activation(out=one[:], in_=one[:], func=ACT.Sqrt)
+
+        w_codes = keep.tile([P, FEATURES], U32, align_bytes=64)
+        w_scales = keep.tile([P, FEATURES], U8, align_bytes=64)
+        h_codes = keep.tile([P, ROWS], U32, align_bytes=64)
+        h_scales = keep.tile([P, ROWS], U8, align_bytes=64)
+
+        def multiply(acc, half, chunk, start, stop):
+            features = slice(half * P, (half + 1) * P)
+            rows = slice(chunk * CHUNK, (chunk + 1) * CHUNK)
+            nc.tensor.matmul_mx(
+                out=acc,
+                lhsT=w_codes[:, features].bitcast(FP8X4),
+                lhsT_scale=w_scales[:, features],
+                rhs=h_codes[:, rows].bitcast(FP8X4),
+                rhs_scale=h_scales[:, rows],
+                start=start,
+                stop=stop,
+            )
+
+        gb = keep.tile([P, 2 * HALVES], F32)
+        neg_pivot = keep.tile([P, HALVES], F32)
+        sq_parts = keep.tile([P, HALVES, CHUNKS], F32)
+        gain = keep.tile([P, HALVES], F32)
+        shift = keep.tile([P, HALVES], F32)
+
+        with tc.psum_pool(name="psum_t", bufs=4) as psum_t, tc.psum_pool(
+            name="psum_y", bufs=2
+        ) as psum_y, tc.psum_pool(name="psum_sum", bufs=1) as psum_sum:
+            wT = psum_y.tile([P, PACK, FEATURES], BF16, tag="y")
+            for half in range(HALVES):
+                for t in range(PACK):
+                    nc.tensor.transpose(
+                        wT[:, t, half * P : (half + 1) * P],
+                        w_rows[:, half, t:K:PACK],
+                        ident_bf16[:],
+                    )
+            w_grouped = keep.tile([P, FEATURES, PACK], BF16, align_bytes=64)
+            nc.vector.tensor_copy(out=w_grouped[:], in_=wT[:].rearrange("q t c -> q c t"))
+            nc.vector.quantize_mx(
+                out=w_codes[:].bitcast(FP8X4),
+                scales=w_scales[:],
+                in_=w_grouped[:].rearrange("q c t -> q (c t)"),
+            )
+
+            gbT = psum_y.tile([P, P], BF16, tag="y")
+            nc.tensor.transpose(gbT[:], gb_rows[:], ident_bf16[:])
+            nc.vector.tensor_copy(out=gb[:], in_=gbT[:, 0 : 2 * HALVES])
+
+            row_sums = [
+                psum_sum.tile([P, CHUNK], F32, name="row_sums%d" % half) for half in range(HALVES)
+            ]
+            xT_banks = {}
+            y_banks = {}
+
+            def transposes(chunk):
+                for pair in range(BLOCKS // PAIR):
+                    xT = psum_t.tile([P, PACK, PAIR * P], BF16, name="xT")
+                    for s in range(PAIR):
+                        for t in range(PACK):
+                            nc.tensor.transpose(
+                                xT[:, t, s * P : (s + 1) * P],
+                                x_tiles[chunk][:, pair * PAIR + s, t:K:PACK],
+                                ident_bf16[:],
+                            )
+                    xT_banks[(chunk, pair)] = xT
+
+            def swish_and_quantise(chunk):
+                grouped = stage.tile([P, CHUNK, PACK], BF16, align_bytes=64)
+                for pair in range(BLOCKS // PAIR):
+                    x_by_row = xT_banks[(chunk, pair)][:].rearrange("q t r -> q r t")
+                    ramp = stage.tile([P, PAIR * P, PACK], F32)
+                    nc.scalar.activation(
+                        out=ramp[:], in_=x_by_row, func=ACT.Relu, scale=1.0 / 6.0, bias=0.5
+                    )
+                    nc.vector.scalar_tensor_tensor(
+                        out=grouped[:, pair * PAIR * P : (pair + 1) * PAIR * P, :],
+                        in0=ramp[:],
+                        scalar=1.0,
+                        in1=x_by_row,
+                        op0=ALU.min,
+                        op1=ALU.mult,
+                    )
+                rows = slice(chunk * CHUNK, (chunk + 1) * CHUNK)
+                nc.vector.quantize_mx(
+                    out=h_codes[:, rows].bitcast(FP8X4),
+                    scales=h_scales[:, rows],
+                    in_=grouped[:].rearrange("q r t -> q (r t)"),
+                )
+
+            def products(chunk):
+                for half in range(HALVES):
+                    y = psum_y.tile([P, CHUNK], F32, name="y")
+                    multiply(y[:], half, chunk, True, True)
+                    multiply(row_sums[half][:], half, chunk, chunk == 0, chunk == CHUNKS - 1)
+                    y_banks[(chunk, half)] = y
+
+            def choose_pivot():
+                first_sum = keep.tile([P, HALVES], F32)
+                for half in range(HALVES):
+                    nc.vector.tensor_reduce(
+                        out=first_sum[:, half : half + 1],
+                        in_=y_banks[(0, half)][:, 0:P],
+                        axis=X_AXIS,
+                        op=ALU.add,
+                    )
+                nc.vector.tensor_scalar_mul(neg_pivot[:], first_sum[:], -1.0 / P)
+
+            def squares(chunk):
+                for half in range(HALVES):
+                    unread = stage.tile([P, CHUNK], BF16)
+                    nc.scalar.activation(
+                        out=unread[:],
+                        in_=y_banks[(chunk, half)][:],
+                        func=ACT.Square,
+                        bias=neg_pivot[:, half : half + 1],
+                        accum_out=sq_parts[:, half, chunk : chunk + 1],
+                    )
+
+            transposes(0)
+            transposes(1)
+            for step in range(CHUNKS + 2):
+                if 1 <= step <= CHUNKS:
+                    products(step - 1)
+                if step == 1:
+                    choose_pivot()
+                if step < CHUNKS:
+                    swish_and_quantise(step)
+                if step >= 2:
+                    squares(step - 2)
+                if step + 2 < CHUNKS:
+                    transposes(step + 2)
+
+            total = keep.tile([P, HALVES], F32)
+            for half in range(HALVES):
+                nc.vector.tensor_reduce(
+                    out=total[:, half : half + 1], in_=row_sums[half][:], axis=X_AXIS, op=ALU.add
+                )
+            sq_total = keep.tile([P, HALVES], F32)
+            nc.vector.tensor_reduce(out=sq_total[:], in_=sq_parts[:], axis=X_AXIS, op=ALU.add)
+            mean = keep.tile([P, HALVES], F32)
+            nc.vector.tensor_scalar_mul(mean[:], total[:], 1.0 / ROWS)
+            off = keep.tile([P, HALVES], F32)
+            nc.vector.tensor_add(out=off[:], in0=mean[:], in1=neg_pivot[:])
+            off_sq = keep.tile([P, HALVES], F32)
+            nc.vector.tensor_mul(out=off_sq[:], in0=off[:], in1=off[:])
+            var = keep.tile([P, HALVES], F32)
+            nc.vector.scalar_tensor_tensor(
+                out=var[:],
+                in0=sq_total[:],
+                scalar=1.0 / ROWS,
+                in1=off_sq[:],
+                op0=ALU.mult,
+                op1=ALU.subtract,
+            )
+            var_eps = keep.tile([P, HALVES], F32)
+            nc.vector.tensor_scalar(
+                out=var_eps[:], in0=var[:], scalar1=0.0, scalar2=EPS, op0=ALU.max, op1=ALU.add
+            )
+            std = keep.tile([P, HALVES], F32)
+            nc.scalar.activation(out=std[:], in_=var_eps[:], func=ACT.Sqrt)
+            rstd = keep.tile([P, HALVES], F32)
+            nc.vector.reciprocal(out=rstd[:], in_=std[:])
+            nc.vector.tensor_mul(out=gain[:], in0=gb[:, 0:HALVES], in1=rstd[:])
+            mean_gain = keep.tile([P, HALVES], F32)
+            nc.vector.tensor_mul(out=mean_gain[:], in0=mean[:], in1=gain[:])
+            nc.vector.tensor_sub(out=shift[:], in0=gb[:, HALVES : 2 * HALVES], in1=mean_gain[:])
+
+        with tc.psum_pool(name="psum_y2", bufs=4, reuse_waits="tile") as psum_y2, tc.psum_pool(
+            name="psum_o", bufs=4, reuse_waits="tile"
+        ) as psum_o:
+            y2_banks = {}
+            normed = {}
+
+            def products_again(chunk):
+                for half in range(HALVES):
+                    y2 = psum_y2.tile([P, CHUNK], F32, name="y2")
+                    multiply(y2[:], half, chunk, True, True)
+                    y2_banks[(chunk, half)] = y2
+
+            def normalise(chunk):
+                normed0 = stage.tile([P, CHUNK], F32)
+                nc.scalar.activation(
+                    out=normed0[:],
+                    in_=y2_banks[(chunk, 0)][:],
+                    func=ACT.Identity,
+                    scale=gain[:, 0:1],
+                    bias=shift[:, 0:1],
+                )
+                normed1 = stage.tile([P, CHUNK], F32)
+                nc.vector.tensor_scalar(
+                    out=normed1[:],
+                    in0=y2_banks[(chunk, 1)][:],
+                    scalar1=gain[:, 1:2],
+                    scalar2=shift[:, 1:2],
+                    op0=ALU.mult,
+                    op1=ALU.add,
+                )
+                normed[(chunk, 0)] = normed0
+                normed[(chunk, 1)] = normed1
+
+            def transpose_back_and_store(chunk):
+                result = stage.tile([P, BLOCKS, FEATURES], F32)
+                for pair in range(BLOCKS // PAIR):
+                    oT = psum_o.tile([P, PAIR, FEATURES], F32)
+                    for s in range(PAIR):
+                        block = pair * PAIR + s
+                        for half in range(HALVES):
+                            nc.tensor.transpose(
+                                oT[:, s, half * P : (half + 1) * P],
+                                normed[(chunk, half)][:, block * P : (block + 1) * P],
+                                ident_f32[:],
+                            )
+                    blocks = slice(pair * PAIR, (pair + 1) * PAIR)
+                    if pair == 0:
+                        nc.scalar.copy(out=result[:, blocks, :], in_=oT[:])
+                    else:
+                        nc.vector.tensor_copy(out=result[:, blocks, :], in_=oT[:])
+                nc.sync.dma_start(out=out_chunks[chunk], in_=result[:])
+
+            products_again(0)
+            products_again(1)
+            normalise(0)
+            for chunk in range(CHUNKS):
+                if chunk + 1 < CHUNKS:
+                    normalise(chunk + 1)
+                transpose_back_and_store(chunk)
+                if chunk + 2 < CHUNKS:
+                    products_again(chunk + 2)

@@ -12,6 +12,9 @@ X_AXIS = mybir.AxisListType.X
 
 P = 128
 PACK = 4
+WORDS = 2
+SIDES = 2
+SIDE = P // SIDES
 K = P * PACK
 ROWS = 32 * 256
 FEATURES = 256
@@ -54,6 +57,10 @@ def tile_attention_pb_t_kernel(tc, h_attn, proj_w, proj_g, proj_b, out):
         make_identity(nc, ident_bf16[:])
         ident_f32 = keep.tile([P, P], F32)
         make_identity(nc, ident_f32[:])
+        ident_sides = keep.tile([P, SIDE, SIDES], F32)
+        nc.vector.tensor_copy(
+            out=ident_sides[:], in_=ident_f32[:].rearrange("i (r j) -> i j r", r=SIDES)
+        )
 
         one = keep.tile([P, 1], F32)
         nc.vector.memset(one[:], 1.0)
@@ -86,20 +93,24 @@ def tile_attention_pb_t_kernel(tc, h_attn, proj_w, proj_g, proj_b, out):
         with tc.psum_pool(name="psum_t", bufs=4) as psum_t, tc.psum_pool(
             name="psum_y", bufs=2
         ) as psum_y, tc.psum_pool(name="psum_sum", bufs=1) as psum_sum:
-            wT = psum_y.tile([P, PACK, FEATURES], BF16, tag="y")
+            wT = psum_y.tile([P, WORDS, FEATURES], F32, tag="y")
             for half in range(HALVES):
-                for t in range(PACK):
+                words = w_rows[:, half, :].bitcast(F32)
+                for u in range(WORDS):
                     nc.tensor.transpose(
-                        wT[:, t, half * P : (half + 1) * P],
-                        w_rows[:, half, t:K:PACK],
-                        ident_bf16[:],
+                        wT[:, u, half * P : (half + 1) * P],
+                        words[:, u : K // 2 : WORDS],
+                        ident_f32[:],
                     )
-            w_grouped = keep.tile([P, FEATURES, PACK], BF16, align_bytes=64)
-            nc.vector.tensor_copy(out=w_grouped[:], in_=wT[:].rearrange("q t c -> q c t"))
+            w_grouped = keep.tile([P, FEATURES * PACK], BF16, align_bytes=64)
+            nc.vector.tensor_copy(
+                out=w_grouped[:].bitcast(F32).rearrange("q (c u) -> q c u", u=WORDS),
+                in_=wT[:].rearrange("q u c -> q c u"),
+            )
             nc.vector.quantize_mx(
                 out=w_codes[:].bitcast(FP8X4),
                 scales=w_scales[:],
-                in_=w_grouped[:].rearrange("q c t -> q (c t)"),
+                in_=w_grouped[:],
             )
 
             gbT = psum_y.tile([P, P], BF16, tag="y")
@@ -114,37 +125,44 @@ def tile_attention_pb_t_kernel(tc, h_attn, proj_w, proj_g, proj_b, out):
 
             def transposes(chunk):
                 for pair in range(BLOCKS // PAIR):
-                    xT = psum_t.tile([P, PACK, PAIR * P], BF16, name="xT")
+                    xT = psum_t.tile([P, PAIR, SIDE, WORDS, SIDES], F32, name="xT")
                     for s in range(PAIR):
-                        for t in range(PACK):
+                        words = x_tiles[chunk][:, pair * PAIR + s, :].bitcast(F32)
+                        for u in range(WORDS):
                             nc.tensor.transpose(
-                                xT[:, t, s * P : (s + 1) * P],
-                                x_tiles[chunk][:, pair * PAIR + s, t:K:PACK],
-                                ident_bf16[:],
+                                xT[:, s, :, u, :],
+                                words[:, u : K // 2 : WORDS],
+                                ident_sides[:],
                             )
                     xT_banks[(chunk, pair)] = xT
 
             def swish_and_quantise(chunk):
-                grouped = stage.tile([P, CHUNK, PACK], BF16, align_bytes=64)
+                grouped = stage.tile([P, BLOCKS, SIDES, SIDE * WORDS, 2], BF16, align_bytes=64)
                 for pair in range(BLOCKS // PAIR):
-                    x_by_row = xT_banks[(chunk, pair)][:].rearrange("q t r -> q r t")
-                    ramp = stage.tile([P, PAIR * P, PACK], F32)
+                    x_by_side = (
+                        xT_banks[(chunk, pair)][:]
+                        .rearrange("q s j u r -> q (s j u r)")
+                        .bitcast(BF16)
+                        .rearrange("q (m r e) -> q r m e", r=SIDES, e=2)
+                    )
+                    ramp = stage.tile([P, SIDES, PAIR * SIDE * WORDS, 2], F32)
                     nc.scalar.activation(
-                        out=ramp[:], in_=x_by_row, func=ACT.Relu, scale=1.0 / 6.0, bias=0.5
+                        out=ramp[:], in_=x_by_side, func=ACT.Relu, scale=1.0 / 6.0, bias=0.5
                     )
-                    nc.vector.scalar_tensor_tensor(
-                        out=grouped[:, pair * PAIR * P : (pair + 1) * PAIR * P, :],
-                        in0=ramp[:],
-                        scalar=1.0,
-                        in1=x_by_row,
-                        op0=ALU.min,
-                        op1=ALU.mult,
-                    )
+                    for side in range(SIDES):
+                        nc.vector.scalar_tensor_tensor(
+                            out=grouped[:, pair * PAIR : (pair + 1) * PAIR, side],
+                            in0=ramp[:, side].rearrange("q (s m) e -> q s m e", s=PAIR),
+                            scalar=1.0,
+                            in1=x_by_side[:, side].rearrange("q (s m) e -> q s m e", s=PAIR),
+                            op0=ALU.min,
+                            op1=ALU.mult,
+                        )
                 rows = slice(chunk * CHUNK, (chunk + 1) * CHUNK)
                 nc.vector.quantize_mx(
                     out=h_codes[:, rows].bitcast(FP8X4),
                     scales=h_scales[:, rows],
-                    in_=grouped[:].rearrange("q r t -> q (r t)"),
+                    in_=grouped[:].rearrange("q b r m e -> q (b r m e)"),
                 )
 
             def products(chunk):

@@ -19,10 +19,11 @@ K = P * PACK
 ROWS = 32 * 256
 FEATURES = 256
 HALVES = FEATURES // P
-CHUNK = 512
-CHUNKS = ROWS // CHUNK
-BLOCKS = CHUNK // P
 PAIR = 2
+CHUNK_BLOCKS = [2] + [4] * 15 + [2]
+CHUNKS = len(CHUNK_BLOCKS)
+MAX_CHUNK = max(CHUNK_BLOCKS) * P
+SUM_WIDTH = PAIR * P
 EPS = 1e-5
 
 FLOPS = 2 * ROWS * K * FEATURES
@@ -31,14 +32,32 @@ FLOPS = 2 * ROWS * K * FEATURES
 def tile_attention_pb_t_kernel(tc, h_attn, proj_w, proj_g, proj_b, out):
     nc = tc.nc
 
-    x_chunks = h_attn.flatten_outer_dims().rearrange("(i p j) k -> i p j k", p=P, j=BLOCKS)
-    out_chunks = out.flatten_outer_dims().rearrange("(i p j) c -> i p j c", p=P, j=BLOCKS)
+    starts = [P * sum(CHUNK_BLOCKS[:i]) for i in range(CHUNKS)]
+    cols = [slice(starts[i], starts[i] + P * CHUNK_BLOCKS[i]) for i in range(CHUNKS)]
+    x_all = h_attn.flatten_outer_dims()
+    out_all = out.flatten_outer_dims()
+    x_chunks = [
+        x_all[cols[i], :].rearrange("(p j) k -> p j k", j=CHUNK_BLOCKS[i]) for i in range(CHUNKS)
+    ]
+    out_chunks = [
+        out_all[cols[i], :].rearrange("(p j) c -> p j c", j=CHUNK_BLOCKS[i]) for i in range(CHUNKS)
+    ]
+    pairs = [CHUNK_BLOCKS[i] // PAIR for i in range(CHUNKS)]
 
     with tc.manual_schedule(), tc.tile_pool(name="keep", bufs=1) as keep, tc.tile_pool(
-        name="loads", bufs=CHUNKS
-    ) as loads, tc.tile_pool(name="stage", bufs=3) as stage:
+        name="stage", bufs=3
+    ) as stage:
+        x_tiles = []
+
+        def load(chunk):
+            x_rows = keep.tile([P, CHUNK_BLOCKS[chunk], K], BF16, name="x_rows%d" % chunk)
+            nc.sync.dma_start(out=x_rows[:], in_=x_chunks[chunk])
+            x_tiles.append(x_rows)
+
+        load(0)
         w_rows = keep.tile([P, HALVES, K], BF16)
         nc.sync.dma_start(out=w_rows[:], in_=proj_w.rearrange("(h c) k -> c h k", h=HALVES))
+        load(1)
         gb_rows = keep.tile([P, P], BF16)
         nc.vector.memset(gb_rows[:], 0.0)
         nc.sync.dma_start(
@@ -47,33 +66,29 @@ def tile_attention_pb_t_kernel(tc, h_attn, proj_w, proj_g, proj_b, out):
         nc.sync.dma_start(
             out=gb_rows[HALVES : 2 * HALVES, :], in_=proj_b.rearrange("(h c) -> h c", h=HALVES)
         )
-        x_tiles = []
-        for chunk in range(CHUNKS):
-            x_rows = loads.tile([P, BLOCKS, K], BF16, name="x_rows")
-            nc.sync.dma_start(out=x_rows[:], in_=x_chunks[chunk])
-            x_tiles.append(x_rows)
+        for chunk in range(2, CHUNKS):
+            load(chunk)
 
-        ident_bf16 = keep.tile([P, P], BF16)
-        make_identity(nc, ident_bf16[:])
         ident_f32 = keep.tile([P, P], F32)
         make_identity(nc, ident_f32[:])
         ident_sides = keep.tile([P, SIDE, SIDES], F32)
         nc.vector.tensor_copy(
             out=ident_sides[:], in_=ident_f32[:].rearrange("i (r j) -> i j r", r=SIDES)
         )
+        ident_bf16 = keep.tile([P, P], BF16)
+        make_identity(nc, ident_bf16[:])
 
         one = keep.tile([P, 1], F32)
         nc.vector.memset(one[:], 1.0)
-        nc.scalar.activation(out=one[:], in_=one[:], func=ACT.Sqrt)
+        nc.scalar.activation(out=one[:], in_=one[:], func=ACT.Abs_reciprocal_sqrt)
 
         w_codes = keep.tile([P, FEATURES], U32, align_bytes=64)
         w_scales = keep.tile([P, FEATURES], U8, align_bytes=64)
         h_codes = keep.tile([P, ROWS], U32, align_bytes=64)
         h_scales = keep.tile([P, ROWS], U8, align_bytes=64)
 
-        def multiply(acc, half, chunk, start, stop):
+        def multiply(acc, half, rows, start, stop):
             features = slice(half * P, (half + 1) * P)
-            rows = slice(chunk * CHUNK, (chunk + 1) * CHUNK)
             nc.tensor.matmul_mx(
                 out=acc,
                 lhsT=w_codes[:, features].bitcast(FP8X4),
@@ -86,45 +101,24 @@ def tile_attention_pb_t_kernel(tc, h_attn, proj_w, proj_g, proj_b, out):
 
         gb = keep.tile([P, 2 * HALVES], F32)
         neg_pivot = keep.tile([P, HALVES], F32)
-        sq_parts = keep.tile([P, HALVES, CHUNKS], F32)
+        pivot = keep.tile([P, HALVES], F32)
+        sq_parts = keep.tile([P, HALVES, CHUNKS - 1], F32)
+        sq_last = keep.tile([P, HALVES], F32)
         gain = keep.tile([P, HALVES], F32)
         shift = keep.tile([P, HALVES], F32)
 
         with tc.psum_pool(name="psum_t", bufs=4) as psum_t, tc.psum_pool(
             name="psum_y", bufs=2
         ) as psum_y, tc.psum_pool(name="psum_sum", bufs=1) as psum_sum:
-            wT = psum_y.tile([P, WORDS, FEATURES], F32, tag="y")
-            for half in range(HALVES):
-                words = w_rows[:, half, :].bitcast(F32)
-                for u in range(WORDS):
-                    nc.tensor.transpose(
-                        wT[:, u, half * P : (half + 1) * P],
-                        words[:, u : K // 2 : WORDS],
-                        ident_f32[:],
-                    )
-            w_grouped = keep.tile([P, FEATURES * PACK], BF16, align_bytes=64)
-            nc.vector.tensor_copy(
-                out=w_grouped[:].bitcast(F32).rearrange("q (c u) -> q c u", u=WORDS),
-                in_=wT[:].rearrange("q u c -> q c u"),
-            )
-            nc.vector.quantize_mx(
-                out=w_codes[:].bitcast(FP8X4),
-                scales=w_scales[:],
-                in_=w_grouped[:],
-            )
-
-            gbT = psum_y.tile([P, P], BF16, tag="y")
-            nc.tensor.transpose(gbT[:], gb_rows[:], ident_bf16[:])
-            nc.vector.tensor_copy(out=gb[:], in_=gbT[:, 0 : 2 * HALVES])
-
             row_sums = [
-                psum_sum.tile([P, CHUNK], F32, name="row_sums%d" % half) for half in range(HALVES)
+                psum_sum.tile([P, SUM_WIDTH], F32, name="row_sums%d" % half)
+                for half in range(HALVES)
             ]
             xT_banks = {}
             y_banks = {}
 
             def transposes(chunk):
-                for pair in range(BLOCKS // PAIR):
+                for pair in range(pairs[chunk]):
                     xT = psum_t.tile([P, PAIR, SIDE, WORDS, SIDES], F32, name="xT")
                     for s in range(PAIR):
                         words = x_tiles[chunk][:, pair * PAIR + s, :].bitcast(F32)
@@ -137,8 +131,13 @@ def tile_attention_pb_t_kernel(tc, h_attn, proj_w, proj_g, proj_b, out):
                     xT_banks[(chunk, pair)] = xT
 
             def swish_and_quantise(chunk):
-                grouped = stage.tile([P, BLOCKS, SIDES, SIDE * WORDS, 2], BF16, align_bytes=64)
-                for pair in range(BLOCKS // PAIR):
+                grouped = stage.tile(
+                    [P, CHUNK_BLOCKS[chunk], SIDES, SIDE * WORDS, 2],
+                    BF16,
+                    name="grouped",
+                    align_bytes=64,
+                )
+                for pair in range(pairs[chunk]):
                     x_by_side = (
                         xT_banks[(chunk, pair)][:]
                         .rearrange("q s j u r -> q (s j u r)")
@@ -158,19 +157,26 @@ def tile_attention_pb_t_kernel(tc, h_attn, proj_w, proj_g, proj_b, out):
                             op0=ALU.min,
                             op1=ALU.mult,
                         )
-                rows = slice(chunk * CHUNK, (chunk + 1) * CHUNK)
                 nc.vector.quantize_mx(
-                    out=h_codes[:, rows].bitcast(FP8X4),
-                    scales=h_scales[:, rows],
+                    out=h_codes[:, cols[chunk]].bitcast(FP8X4),
+                    scales=h_scales[:, cols[chunk]],
                     in_=grouped[:].rearrange("q b r m e -> q (b r m e)"),
                 )
 
             def products(chunk):
                 for half in range(HALVES):
-                    y = psum_y.tile([P, CHUNK], F32, name="y")
-                    multiply(y[:], half, chunk, True, True)
-                    multiply(row_sums[half][:], half, chunk, chunk == 0, chunk == CHUNKS - 1)
+                    y = psum_y.tile([P, CHUNK_BLOCKS[chunk] * P], F32, name="y")
+                    multiply(y[:], half, cols[chunk], True, True)
                     y_banks[(chunk, half)] = y
+                    for pair in range(pairs[chunk]):
+                        first = starts[chunk] + pair * SUM_WIDTH
+                        multiply(
+                            row_sums[half][:],
+                            half,
+                            slice(first, first + SUM_WIDTH),
+                            first == 0,
+                            first == ROWS - SUM_WIDTH,
+                        )
 
             def choose_pivot():
                 first_sum = keep.tile([P, HALVES], F32)
@@ -182,20 +188,46 @@ def tile_attention_pb_t_kernel(tc, h_attn, proj_w, proj_g, proj_b, out):
                         op=ALU.add,
                     )
                 nc.vector.tensor_scalar_mul(neg_pivot[:], first_sum[:], -1.0 / P)
+                nc.vector.tensor_scalar_mul(pivot[:], first_sum[:], 1.0 / P)
 
             def squares(chunk):
                 for half in range(HALVES):
-                    unread = stage.tile([P, CHUNK], BF16)
+                    unread = stage.tile([P, MAX_CHUNK], BF16)
+                    if chunk < CHUNKS - 1:
+                        sum_of_squares = sq_parts[:, half, chunk : chunk + 1]
+                    else:
+                        sum_of_squares = sq_last[:, half : half + 1]
                     nc.scalar.activation(
-                        out=unread[:],
+                        out=unread[:, 0 : CHUNK_BLOCKS[chunk] * P],
                         in_=y_banks[(chunk, half)][:],
                         func=ACT.Square,
                         bias=neg_pivot[:, half : half + 1],
-                        accum_out=sq_parts[:, half, chunk : chunk + 1],
+                        accum_out=sum_of_squares,
                     )
 
             transposes(0)
+
+            wT = psum_y.tile([P, WORDS, FEATURES], F32, tag="y")
+            for half in range(HALVES):
+                words = w_rows[:, half, :].bitcast(F32)
+                for u in range(WORDS):
+                    nc.tensor.transpose(
+                        wT[:, u, half * P : (half + 1) * P],
+                        words[:, u : K // 2 : WORDS],
+                        ident_f32[:],
+                    )
+            w_grouped = keep.tile([P, FEATURES * PACK], BF16, align_bytes=64)
+            nc.vector.tensor_copy(
+                out=w_grouped[:].bitcast(F32).rearrange("q (c u) -> q c u", u=WORDS),
+                in_=wT[:].rearrange("q u c -> q c u"),
+            )
+            nc.vector.quantize_mx(
+                out=w_codes[:].bitcast(FP8X4), scales=w_scales[:], in_=w_grouped[:]
+            )
             transposes(1)
+            gbT = psum_y.tile([P, P], BF16, tag="y")
+            nc.tensor.transpose(gbT[:], gb_rows[:], ident_bf16[:])
+            nc.vector.tensor_copy(out=gb[:], in_=gbT[:, 0 : 2 * HALVES])
             for step in range(CHUNKS + 2):
                 if 1 <= step <= CHUNKS:
                     products(step - 1)
@@ -208,40 +240,74 @@ def tile_attention_pb_t_kernel(tc, h_attn, proj_w, proj_g, proj_b, out):
                 if step + 2 < CHUNKS:
                     transposes(step + 2)
 
+            sq_total = keep.tile([P, HALVES], F32)
+            nc.vector.tensor_reduce(out=sq_total[:], in_=sq_parts[:], axis=X_AXIS, op=ALU.add)
+            sq_mean = keep.tile([P, HALVES], F32)
+            nc.vector.tensor_scalar(
+                out=sq_mean[:],
+                in0=sq_total[:],
+                scalar1=1.0 / ROWS,
+                scalar2=EPS,
+                op0=ALU.mult,
+                op1=ALU.add,
+            )
             total = keep.tile([P, HALVES], F32)
             for half in range(HALVES):
                 nc.vector.tensor_reduce(
                     out=total[:, half : half + 1], in_=row_sums[half][:], axis=X_AXIS, op=ALU.add
                 )
-            sq_total = keep.tile([P, HALVES], F32)
-            nc.vector.tensor_reduce(out=sq_total[:], in_=sq_parts[:], axis=X_AXIS, op=ALU.add)
-            mean = keep.tile([P, HALVES], F32)
-            nc.vector.tensor_scalar_mul(mean[:], total[:], 1.0 / ROWS)
-            off = keep.tile([P, HALVES], F32)
-            nc.vector.tensor_add(out=off[:], in0=mean[:], in1=neg_pivot[:])
+            neg_mean = keep.tile([P, HALVES], F32)
+            nc.vector.tensor_scalar_mul(neg_mean[:], total[:], -1.0 / ROWS)
+
+            def each_half(result, **args):
+                for half in range(HALVES):
+                    column = slice(half, half + 1)
+                    nc.scalar.activation(
+                        out=result[:, column],
+                        func=args["func"],
+                        in_=args["in_"][:, column],
+                        scale=args["scale"](column),
+                        bias=args["bias"](column),
+                    )
+
+            sq_eps = keep.tile([P, HALVES], F32)
+            each_half(
+                sq_eps,
+                func=ACT.Identity,
+                in_=sq_last,
+                scale=lambda c: 1.0 / ROWS,
+                bias=lambda c: sq_mean[:, c],
+            )
             off_sq = keep.tile([P, HALVES], F32)
-            nc.vector.tensor_mul(out=off_sq[:], in0=off[:], in1=off[:])
-            var = keep.tile([P, HALVES], F32)
-            nc.vector.scalar_tensor_tensor(
-                out=var[:],
-                in0=sq_total[:],
-                scalar=1.0 / ROWS,
-                in1=off_sq[:],
-                op0=ALU.mult,
-                op1=ALU.subtract,
+            each_half(
+                off_sq,
+                func=ACT.Square,
+                in_=total,
+                scale=lambda c: -1.0 / ROWS,
+                bias=lambda c: pivot[:, c],
             )
-            var_eps = keep.tile([P, HALVES], F32)
-            nc.vector.tensor_scalar(
-                out=var_eps[:], in0=var[:], scalar1=0.0, scalar2=EPS, op0=ALU.max, op1=ALU.add
-            )
-            std = keep.tile([P, HALVES], F32)
-            nc.scalar.activation(out=std[:], in_=var_eps[:], func=ACT.Sqrt)
             rstd = keep.tile([P, HALVES], F32)
-            nc.vector.reciprocal(out=rstd[:], in_=std[:])
-            nc.vector.tensor_mul(out=gain[:], in0=gb[:, 0:HALVES], in1=rstd[:])
-            mean_gain = keep.tile([P, HALVES], F32)
-            nc.vector.tensor_mul(out=mean_gain[:], in0=mean[:], in1=gain[:])
-            nc.vector.tensor_sub(out=shift[:], in0=gb[:, HALVES : 2 * HALVES], in1=mean_gain[:])
+            each_half(
+                rstd,
+                func=ACT.Abs_reciprocal_sqrt,
+                in_=off_sq,
+                scale=lambda c: -1.0,
+                bias=lambda c: sq_eps[:, c],
+            )
+            each_half(
+                gain,
+                func=ACT.Identity,
+                in_=gb,
+                scale=lambda c: rstd[:, c],
+                bias=lambda c: 0.0,
+            )
+            each_half(
+                shift,
+                func=ACT.Identity,
+                in_=neg_mean,
+                scale=lambda c: gain[:, c],
+                bias=lambda c: gb[:, slice(HALVES + c.start, HALVES + c.stop)],
+            )
 
         with tc.psum_pool(name="psum_y2", bufs=4, reuse_waits="tile") as psum_y2, tc.psum_pool(
             name="psum_o", bufs=4, reuse_waits="tile"
@@ -251,22 +317,23 @@ def tile_attention_pb_t_kernel(tc, h_attn, proj_w, proj_g, proj_b, out):
 
             def products_again(chunk):
                 for half in range(HALVES):
-                    y2 = psum_y2.tile([P, CHUNK], F32, name="y2")
-                    multiply(y2[:], half, chunk, True, True)
+                    y2 = psum_y2.tile([P, CHUNK_BLOCKS[chunk] * P], F32, name="y2")
+                    multiply(y2[:], half, cols[chunk], True, True)
                     y2_banks[(chunk, half)] = y2
 
             def normalise(chunk):
-                normed0 = stage.tile([P, CHUNK], F32)
+                rows = CHUNK_BLOCKS[chunk] * P
+                normed0 = stage.tile([P, MAX_CHUNK], F32)
                 nc.scalar.activation(
-                    out=normed0[:],
+                    out=normed0[:, 0:rows],
                     in_=y2_banks[(chunk, 0)][:],
                     func=ACT.Identity,
                     scale=gain[:, 0:1],
                     bias=shift[:, 0:1],
                 )
-                normed1 = stage.tile([P, CHUNK], F32)
+                normed1 = stage.tile([P, MAX_CHUNK], F32)
                 nc.vector.tensor_scalar(
-                    out=normed1[:],
+                    out=normed1[:, 0:rows],
                     in0=y2_banks[(chunk, 1)][:],
                     scalar1=gain[:, 1:2],
                     scalar2=shift[:, 1:2],
@@ -277,8 +344,8 @@ def tile_attention_pb_t_kernel(tc, h_attn, proj_w, proj_g, proj_b, out):
                 normed[(chunk, 1)] = normed1
 
             def transpose_back_and_store(chunk):
-                result = stage.tile([P, BLOCKS, FEATURES], F32)
-                for pair in range(BLOCKS // PAIR):
+                result = stage.tile([P, CHUNK_BLOCKS[chunk], FEATURES], F32, name="result")
+                for pair in range(pairs[chunk]):
                     oT = psum_o.tile([P, PAIR, FEATURES], F32)
                     for s in range(PAIR):
                         block = pair * PAIR + s

@@ -115,11 +115,24 @@ def tile_attention_pb_t_kernel(tc, h_attn, proj_w, proj_g, proj_b, out):
                 for half in range(HALVES)
             ]
             xT_banks = {}
+            h_rows = {}
             y_banks = {}
 
             def transposes(chunk):
                 for pair in range(pairs[chunk]):
-                    xT = psum_t.tile([P, PAIR, SIDE, WORDS, SIDES], F32, name="xT")
+                    if (chunk, pair) in h_rows:
+                        hT = psum_t.tile([P, WORDS, PAIR * P], F32, tag="xT", name="hT")
+                        for s in range(PAIR):
+                            words = h_rows[(chunk, pair)][:, s, :].bitcast(F32)
+                            for u in range(WORDS):
+                                nc.tensor.transpose(
+                                    hT[:, u, s * P : (s + 1) * P],
+                                    words[:, u : K // 2 : WORDS],
+                                    ident_f32[:],
+                                )
+                        xT_banks[(chunk, pair)] = hT
+                        continue
+                    xT = psum_t.tile([P, PAIR, SIDE, WORDS, SIDES], F32, tag="xT", name="xT")
                     for s in range(PAIR):
                         words = x_tiles[chunk][:, pair * PAIR + s, :].bitcast(F32)
                         for u in range(WORDS):
@@ -130,6 +143,25 @@ def tile_attention_pb_t_kernel(tc, h_attn, proj_w, proj_g, proj_b, out):
                             )
                     xT_banks[(chunk, pair)] = xT
 
+            def swish_rows(chunk, pair):
+                v = x_tiles[chunk][:, pair * PAIR : (pair + 1) * PAIR, :]
+                clipped = stage.tile([P, PAIR, K], BF16)
+                nc.vector.tensor_scalar(
+                    out=clipped[:], in0=v, scalar1=-3.0, scalar2=3.0, op0=ALU.max, op1=ALU.min
+                )
+                ramp_rows = stage.tile([P, PAIR, K], F32)
+                nc.gpsimd.tensor_scalar(
+                    out=ramp_rows[:],
+                    in0=clipped[:],
+                    scalar1=3.0,
+                    scalar2=1.0 / 6.0,
+                    op0=ALU.add,
+                    op1=ALU.mult,
+                )
+                h = keep.tile([P, PAIR, K], BF16, name="h_rows%d_%d" % (chunk, pair))
+                nc.gpsimd.tensor_tensor(out=h[:], in0=ramp_rows[:], in1=v, op=ALU.mult)
+                h_rows[(chunk, pair)] = h
+
             def swish_and_quantise(chunk):
                 grouped = stage.tile(
                     [P, CHUNK_BLOCKS[chunk], SIDES, SIDE * WORDS, 2],
@@ -138,6 +170,15 @@ def tile_attention_pb_t_kernel(tc, h_attn, proj_w, proj_g, proj_b, out):
                     align_bytes=64,
                 )
                 for pair in range(pairs[chunk]):
+                    if (chunk, pair) in h_rows:
+                        nc.vector.tensor_copy(
+                            out=grouped[:, pair * PAIR : (pair + 1) * PAIR]
+                            .rearrange("q b r m e -> q (b r m e)")
+                            .bitcast(F32)
+                            .rearrange("q (c u) -> q c u", u=WORDS),
+                            in_=xT_banks[(chunk, pair)][:].rearrange("q u c -> q c u"),
+                        )
+                        continue
                     x_by_side = (
                         xT_banks[(chunk, pair)][:]
                         .rearrange("q s j u r -> q (s j u r)")
@@ -235,6 +276,8 @@ def tile_attention_pb_t_kernel(tc, h_attn, proj_w, proj_g, proj_b, out):
                     choose_pivot()
                 if step < CHUNKS:
                     swish_and_quantise(step)
+                if step % 2 == 0 and step + 4 < CHUNKS - 1:
+                    swish_rows(step + 4, 1)
                 if step >= 2:
                     squares(step - 2)
                 if step + 2 < CHUNKS:

@@ -143,13 +143,15 @@ def tile_attention_pb_t_kernel(tc, h_attn, proj_w, proj_g, proj_b, out):
                             )
                     xT_banks[(chunk, pair)] = xT
 
-            def swish_rows(chunk, pair):
-                v = x_tiles[chunk][:, pair * PAIR : (pair + 1) * PAIR, :]
-                clipped = stage.tile([P, PAIR, K], BF16)
+            def swish_rows(chunk, s):
+                if s == 0:
+                    h_rows[(chunk, 1)] = stage.tile([P, PAIR, K], BF16, name="h_pair")
+                v = x_tiles[chunk][:, PAIR + s, :]
+                clipped = stage.tile([P, K], BF16)
                 nc.vector.tensor_scalar(
                     out=clipped[:], in0=v, scalar1=-3.0, scalar2=3.0, op0=ALU.max, op1=ALU.min
                 )
-                ramp_rows = stage.tile([P, PAIR, K], F32)
+                ramp_rows = stage.tile([P, K], F32)
                 nc.gpsimd.tensor_scalar(
                     out=ramp_rows[:],
                     in0=clipped[:],
@@ -158,9 +160,9 @@ def tile_attention_pb_t_kernel(tc, h_attn, proj_w, proj_g, proj_b, out):
                     op0=ALU.add,
                     op1=ALU.mult,
                 )
-                h = keep.tile([P, PAIR, K], BF16, name="h_rows%d_%d" % (chunk, pair))
-                nc.gpsimd.tensor_tensor(out=h[:], in0=ramp_rows[:], in1=v, op=ALU.mult)
-                h_rows[(chunk, pair)] = h
+                nc.gpsimd.tensor_tensor(
+                    out=h_rows[(chunk, 1)][:, s, :], in0=ramp_rows[:], in1=v, op=ALU.mult
+                )
 
             def swish_and_quantise(chunk):
                 grouped = stage.tile(
@@ -276,7 +278,9 @@ def tile_attention_pb_t_kernel(tc, h_attn, proj_w, proj_g, proj_b, out):
                     choose_pivot()
                 if step < CHUNKS:
                     swish_and_quantise(step)
-                if step % 2 == 0 and step + 4 < CHUNKS - 1:
+                if step % 2 == 1 and step + 5 < CHUNKS - 1:
+                    swish_rows(step + 5, 0)
+                if step % 2 == 0 and 6 <= step + 4 < CHUNKS - 1:
                     swish_rows(step + 4, 1)
                 if step >= 2:
                     squares(step - 2)

@@ -23,6 +23,8 @@ PAIR = 2
 CHUNK_BLOCKS = [2] + [4] * 15 + [2]
 CHUNKS = len(CHUNK_BLOCKS)
 MAX_CHUNK = max(CHUNK_BLOCKS) * P
+GP_CHUNKS = [6, 8, 10, 12, 14, 15]
+GP_BLOCKS = {1 + i: (GP_CHUNKS[i // 2], i % 2) for i in range(2 * len(GP_CHUNKS))}
 SUM_WIDTH = PAIR * P
 EPS = 1e-5
 
@@ -164,46 +166,61 @@ def tile_attention_pb_t_kernel(tc, h_attn, proj_w, proj_g, proj_b, out):
                     out=h_rows[(chunk, 1)][:, s, :], in0=ramp_rows[:], in1=v, op=ALU.mult
                 )
 
-            def swish_and_quantise(chunk):
-                grouped = stage.tile(
-                    [P, CHUNK_BLOCKS[chunk], SIDES, SIDE * WORDS, 2],
-                    BF16,
-                    name="grouped",
-                    align_bytes=64,
+            ramps = {}
+            grouped = {}
+
+            def by_side(chunk, pair):
+                return (
+                    xT_banks[(chunk, pair)][:]
+                    .rearrange("q s j u r -> q (s j u r)")
+                    .bitcast(BF16)
+                    .rearrange("q (m r e) -> q r m e", r=SIDES, e=2)
                 )
+
+            def make_ramps(chunk):
                 for pair in range(pairs[chunk]):
-                    if (chunk, pair) in h_rows:
-                        nc.vector.tensor_copy(
-                            out=grouped[:, pair * PAIR : (pair + 1) * PAIR]
-                            .rearrange("q b r m e -> q (b r m e)")
-                            .bitcast(F32)
-                            .rearrange("q (c u) -> q c u", u=WORDS),
-                            in_=xT_banks[(chunk, pair)][:].rearrange("q u c -> q c u"),
+                    if (chunk, pair) not in h_rows:
+                        ramp = stage.tile([P, SIDES, PAIR * SIDE * WORDS, 2], F32)
+                        nc.scalar.activation(
+                            out=ramp[:],
+                            in_=by_side(chunk, pair),
+                            func=ACT.Relu,
+                            scale=1.0 / 6.0,
+                            bias=0.5,
                         )
-                        continue
-                    x_by_side = (
-                        xT_banks[(chunk, pair)][:]
-                        .rearrange("q s j u r -> q (s j u r)")
-                        .bitcast(BF16)
-                        .rearrange("q (m r e) -> q r m e", r=SIDES, e=2)
+                        ramps[(chunk, pair)] = ramp
+
+            def multiply_side(chunk, pair, side):
+                if pair == 0 and side == 0:
+                    grouped[chunk] = stage.tile(
+                        [P, CHUNK_BLOCKS[chunk], SIDES, SIDE * WORDS, 2],
+                        BF16,
+                        name="grouped",
+                        align_bytes=64,
                     )
-                    ramp = stage.tile([P, SIDES, PAIR * SIDE * WORDS, 2], F32)
-                    nc.scalar.activation(
-                        out=ramp[:], in_=x_by_side, func=ACT.Relu, scale=1.0 / 6.0, bias=0.5
-                    )
-                    for side in range(SIDES):
-                        nc.vector.scalar_tensor_tensor(
-                            out=grouped[:, pair * PAIR : (pair + 1) * PAIR, side],
-                            in0=ramp[:, side].rearrange("q (s m) e -> q s m e", s=PAIR),
-                            scalar=1.0,
-                            in1=x_by_side[:, side].rearrange("q (s m) e -> q s m e", s=PAIR),
-                            op0=ALU.min,
-                            op1=ALU.mult,
-                        )
+                nc.vector.scalar_tensor_tensor(
+                    out=grouped[chunk][:, pair * PAIR : (pair + 1) * PAIR, side],
+                    in0=ramps[(chunk, pair)][:, side].rearrange("q (s m) e -> q s m e", s=PAIR),
+                    scalar=1.0,
+                    in1=by_side(chunk, pair)[:, side].rearrange("q (s m) e -> q s m e", s=PAIR),
+                    op0=ALU.min,
+                    op1=ALU.mult,
+                )
+
+            def take_rows(chunk, pair):
+                nc.vector.tensor_copy(
+                    out=grouped[chunk][:, pair * PAIR : (pair + 1) * PAIR]
+                    .rearrange("q b r m e -> q (b r m e)")
+                    .bitcast(F32)
+                    .rearrange("q (c u) -> q c u", u=WORDS),
+                    in_=xT_banks[(chunk, pair)][:].rearrange("q u c -> q c u"),
+                )
+
+            def quantise(chunk):
                 nc.vector.quantize_mx(
                     out=h_codes[:, cols[chunk]].bitcast(FP8X4),
                     scales=h_scales[:, cols[chunk]],
-                    in_=grouped[:].rearrange("q b r m e -> q (b r m e)"),
+                    in_=grouped[chunk][:].rearrange("q b r m e -> q (b r m e)"),
                 )
 
             def products(chunk):
@@ -272,16 +289,24 @@ def tile_attention_pb_t_kernel(tc, h_attn, proj_w, proj_g, proj_b, out):
             nc.tensor.transpose(gbT[:], gb_rows[:], ident_bf16[:])
             nc.vector.tensor_copy(out=gb[:], in_=gbT[:, 0 : 2 * HALVES])
             for step in range(CHUNKS + 2):
+                if step < CHUNKS:
+                    make_ramps(step)
+                    multiply_side(step, 0, 0)
                 if 1 <= step <= CHUNKS:
+                    if step - 1 in GP_BLOCKS:
+                        swish_rows(*GP_BLOCKS[step - 1])
+                    quantise(step - 1)
                     products(step - 1)
+                if step < CHUNKS:
+                    multiply_side(step, 0, 1)
+                    if pairs[step] > 1:
+                        if (step, 1) in h_rows:
+                            take_rows(step, 1)
+                        else:
+                            multiply_side(step, 1, 0)
+                            multiply_side(step, 1, 1)
                 if step == 1:
                     choose_pivot()
-                if step < CHUNKS:
-                    swish_and_quantise(step)
-                if step % 2 == 1 and step + 5 < CHUNKS - 1:
-                    swish_rows(step + 5, 0)
-                if step % 2 == 0 and 6 <= step + 4 < CHUNKS - 1:
-                    swish_rows(step + 4, 1)
                 if step >= 2:
                     squares(step - 2)
                 if step + 2 < CHUNKS:
@@ -356,58 +381,105 @@ def tile_attention_pb_t_kernel(tc, h_attn, proj_w, proj_g, proj_b, out):
                 bias=lambda c: gb[:, slice(HALVES + c.start, HALVES + c.stop)],
             )
 
-        with tc.psum_pool(name="psum_y2", bufs=4, reuse_waits="tile") as psum_y2, tc.psum_pool(
-            name="psum_o", bufs=4, reuse_waits="tile"
-        ) as psum_o:
+        with tc.psum_pool(name="psum_y2", bufs=3, reuse_waits="tile") as psum_y2, tc.psum_pool(
+            name="psum_o", bufs=2, reuse_waits="tile"
+        ) as psum_o, tc.psum_pool(name="psum_r", bufs=3, reuse_waits="tile") as psum_r:
             y2_banks = {}
+            yR_banks = {}
             normed = {}
+            results = {}
+            rows_gs = keep.tile([P, 2, P], F32)
+            last_half = HALVES - 1
+
+            def spread_gain_and_shift():
+                spread = psum_o.tile([P, 2, P], F32, tag="oT", name="spread")
+                for which, numbers in enumerate((gain, shift)):
+                    nc.tensor.matmul(
+                        spread[:, which, :],
+                        lhsT=numbers[:, last_half:HALVES].to_broadcast([P, P]),
+                        rhs=ident_f32[:],
+                        start=True,
+                        stop=True,
+                    )
+                nc.vector.tensor_copy(out=rows_gs[:], in_=spread[:])
 
             def products_again(chunk):
-                for half in range(HALVES):
-                    y2 = psum_y2.tile([P, CHUNK_BLOCKS[chunk] * P], F32, name="y2")
+                blocks = CHUNK_BLOCKS[chunk]
+                for half in range(HALVES if chunk == 0 else 1):
+                    y2 = psum_y2.tile([P, blocks * P], F32, name="y2")
                     multiply(y2[:], half, cols[chunk], True, True)
                     y2_banks[(chunk, half)] = y2
+                if chunk > 0:
+                    yR = psum_r.tile([P, blocks, P], F32, name="yR")
+                    features = slice(last_half * P, HALVES * P)
+                    for block in range(blocks):
+                        rows = slice(starts[chunk] + block * P, starts[chunk] + (block + 1) * P)
+                        nc.tensor.matmul_mx(
+                            out=yR[:, block, :],
+                            lhsT=h_codes[:, rows].bitcast(FP8X4),
+                            lhsT_scale=h_scales[:, rows],
+                            rhs=w_codes[:, features].bitcast(FP8X4),
+                            rhs_scale=w_scales[:, features],
+                            start=True,
+                            stop=True,
+                        )
+                    yR_banks[chunk] = yR
 
             def normalise(chunk):
-                rows = CHUNK_BLOCKS[chunk] * P
-                normed0 = stage.tile([P, MAX_CHUNK], F32)
-                nc.scalar.activation(
-                    out=normed0[:, 0:rows],
-                    in_=y2_banks[(chunk, 0)][:],
-                    func=ACT.Identity,
-                    scale=gain[:, 0:1],
-                    bias=shift[:, 0:1],
+                blocks = CHUNK_BLOCKS[chunk]
+                results[chunk] = stage.tile([P, blocks, FEATURES], F32, name="result", bufs=6)
+                for half in range(HALVES if chunk == 0 else 1):
+                    column = slice(half, half + 1)
+                    normed_half = stage.tile([P, MAX_CHUNK], F32, name="normed%d" % half)
+                    if half == 0:
+                        nc.scalar.activation(
+                            out=normed_half[:, 0 : blocks * P],
+                            in_=y2_banks[(chunk, half)][:],
+                            func=ACT.Identity,
+                            scale=gain[:, column],
+                            bias=shift[:, column],
+                        )
+                    else:
+                        nc.vector.tensor_scalar(
+                            out=normed_half[:, 0 : blocks * P],
+                            in0=y2_banks[(chunk, half)][:],
+                            scalar1=gain[:, column],
+                            scalar2=shift[:, column],
+                            op0=ALU.mult,
+                            op1=ALU.add,
+                        )
+                    normed[(chunk, half)] = normed_half
+
+            def normalise_rows(chunk):
+                blocks = CHUNK_BLOCKS[chunk]
+                scaled = stage.tile([P, blocks, P], F32, name="scaled")
+                nc.vector.tensor_tensor(
+                    out=scaled[:],
+                    in0=yR_banks[chunk][:],
+                    in1=rows_gs[:, 0:1, :].to_broadcast([P, blocks, P]),
+                    op=ALU.mult,
                 )
-                normed1 = stage.tile([P, MAX_CHUNK], F32)
-                nc.vector.tensor_scalar(
-                    out=normed1[:, 0:rows],
-                    in0=y2_banks[(chunk, 1)][:],
-                    scalar1=gain[:, 1:2],
-                    scalar2=shift[:, 1:2],
-                    op0=ALU.mult,
-                    op1=ALU.add,
+                engine = nc.vector if chunk % 3 == 1 else nc.gpsimd
+                engine.tensor_tensor(
+                    out=results[chunk][:, :, last_half * P : HALVES * P],
+                    in0=scaled[:],
+                    in1=rows_gs[:, 1:2, :].to_broadcast([P, blocks, P]),
+                    op=ALU.add,
                 )
-                normed[(chunk, 0)] = normed0
-                normed[(chunk, 1)] = normed1
 
             def transpose_back_and_store(chunk):
-                result = stage.tile([P, CHUNK_BLOCKS[chunk], FEATURES], F32, name="result")
-                for pair in range(pairs[chunk]):
-                    oT = psum_o.tile([P, PAIR, FEATURES], F32)
-                    for s in range(PAIR):
-                        block = pair * PAIR + s
-                        for half in range(HALVES):
-                            nc.tensor.transpose(
-                                oT[:, s, half * P : (half + 1) * P],
-                                normed[(chunk, half)][:, block * P : (block + 1) * P],
-                                ident_f32[:],
-                            )
-                    blocks = slice(pair * PAIR, (pair + 1) * PAIR)
-                    if pair == 0:
-                        nc.scalar.copy(out=result[:, blocks, :], in_=oT[:])
-                    else:
-                        nc.vector.tensor_copy(out=result[:, blocks, :], in_=oT[:])
-                nc.sync.dma_start(out=out_chunks[chunk], in_=result[:])
+                blocks = CHUNK_BLOCKS[chunk]
+                halves = HALVES if chunk == 0 else 1
+                oT = psum_o.tile([P, blocks, halves * P], F32, tag="oT", name="oT")
+                for block in range(blocks):
+                    for half in range(halves):
+                        nc.tensor.transpose(
+                            oT[:, block, half * P : (half + 1) * P],
+                            normed[(chunk, half)][:, block * P : (block + 1) * P],
+                            ident_f32[:],
+                        )
+                nc.scalar.copy(out=results[chunk][:, :, 0 : halves * P], in_=oT[:])
+                nc.sync.dma_start(out=out_chunks[chunk], in_=results[chunk][:])
 
             products_again(0)
             products_again(1)
@@ -416,5 +488,9 @@ def tile_attention_pb_t_kernel(tc, h_attn, proj_w, proj_g, proj_b, out):
                 if chunk + 1 < CHUNKS:
                     normalise(chunk + 1)
                 transpose_back_and_store(chunk)
+                if chunk == 0:
+                    spread_gain_and_shift()
+                if chunk + 1 < CHUNKS:
+                    normalise_rows(chunk + 1)
                 if chunk + 2 < CHUNKS:
                     products_again(chunk + 2)

@@ -23,8 +23,8 @@ PAIR = 2
 CHUNK_BLOCKS = [2] + [4] * 15 + [2]
 CHUNKS = len(CHUNK_BLOCKS)
 MAX_CHUNK = max(CHUNK_BLOCKS) * P
-GP_CHUNKS = [6, 8, 10, 12, 14, 15]
-GP_BLOCKS = {1 + i: (GP_CHUNKS[i // 2], i % 2) for i in range(2 * len(GP_CHUNKS))}
+GP_LEAD = 3
+GP_FIRST = GP_LEAD
 SUM_WIDTH = PAIR * P
 EPS = 1e-5
 
@@ -120,23 +120,18 @@ def tile_attention_pb_t_kernel(tc, h_attn, proj_w, proj_g, proj_b, out):
             h_rows = {}
             y_banks = {}
 
+            def by_gpsimd(chunk, block):
+                return chunk >= GP_FIRST and block == CHUNK_BLOCKS[chunk] - 1
+
             def transposes(chunk):
                 for pair in range(pairs[chunk]):
-                    if (chunk, pair) in h_rows:
-                        hT = psum_t.tile([P, WORDS, PAIR * P], F32, tag="xT", name="hT")
-                        for s in range(PAIR):
-                            words = h_rows[(chunk, pair)][:, s, :].bitcast(F32)
-                            for u in range(WORDS):
-                                nc.tensor.transpose(
-                                    hT[:, u, s * P : (s + 1) * P],
-                                    words[:, u : K // 2 : WORDS],
-                                    ident_f32[:],
-                                )
-                        xT_banks[(chunk, pair)] = hT
-                        continue
                     xT = psum_t.tile([P, PAIR, SIDE, WORDS, SIDES], F32, tag="xT", name="xT")
                     for s in range(PAIR):
-                        words = x_tiles[chunk][:, pair * PAIR + s, :].bitcast(F32)
+                        block = pair * PAIR + s
+                        if by_gpsimd(chunk, block):
+                            words = h_rows[chunk][:].bitcast(F32)
+                        else:
+                            words = x_tiles[chunk][:, block, :].bitcast(F32)
                         for u in range(WORDS):
                             nc.tensor.transpose(
                                 xT[:, s, :, u, :],
@@ -145,10 +140,8 @@ def tile_attention_pb_t_kernel(tc, h_attn, proj_w, proj_g, proj_b, out):
                             )
                     xT_banks[(chunk, pair)] = xT
 
-            def swish_rows(chunk, s):
-                if s == 0:
-                    h_rows[(chunk, 1)] = stage.tile([P, PAIR, K], BF16, name="h_pair")
-                v = x_tiles[chunk][:, PAIR + s, :]
+            def swish_rows(chunk):
+                v = x_tiles[chunk][:, CHUNK_BLOCKS[chunk] - 1, :]
                 clipped = stage.tile([P, K], BF16)
                 nc.vector.tensor_scalar(
                     out=clipped[:], in0=v, scalar1=-3.0, scalar2=3.0, op0=ALU.max, op1=ALU.min
@@ -162,16 +155,16 @@ def tile_attention_pb_t_kernel(tc, h_attn, proj_w, proj_g, proj_b, out):
                     op0=ALU.add,
                     op1=ALU.mult,
                 )
-                nc.gpsimd.tensor_tensor(
-                    out=h_rows[(chunk, 1)][:, s, :], in0=ramp_rows[:], in1=v, op=ALU.mult
-                )
+                h_rows[chunk] = stage.tile([P, K], BF16, name="h_block")
+                nc.gpsimd.tensor_tensor(out=h_rows[chunk][:], in0=ramp_rows[:], in1=v, op=ALU.mult)
 
             ramps = {}
             grouped = {}
 
             def by_side(chunk, pair):
-                return (
-                    xT_banks[(chunk, pair)][:]
+                blocks = PAIR - by_gpsimd(chunk, (pair + 1) * PAIR - 1)
+                return blocks, (
+                    xT_banks[(chunk, pair)][:, 0:blocks]
                     .rearrange("q s j u r -> q (s j u r)")
                     .bitcast(BF16)
                     .rearrange("q (m r e) -> q r m e", r=SIDES, e=2)
@@ -179,16 +172,12 @@ def tile_attention_pb_t_kernel(tc, h_attn, proj_w, proj_g, proj_b, out):
 
             def make_ramps(chunk):
                 for pair in range(pairs[chunk]):
-                    if (chunk, pair) not in h_rows:
-                        ramp = stage.tile([P, SIDES, PAIR * SIDE * WORDS, 2], F32)
-                        nc.scalar.activation(
-                            out=ramp[:],
-                            in_=by_side(chunk, pair),
-                            func=ACT.Relu,
-                            scale=1.0 / 6.0,
-                            bias=0.5,
-                        )
-                        ramps[(chunk, pair)] = ramp
+                    blocks, values = by_side(chunk, pair)
+                    ramp = stage.tile([P, SIDES, blocks * SIDE * WORDS, 2], F32, name="ramp")
+                    nc.scalar.activation(
+                        out=ramp[:], in_=values, func=ACT.Relu, scale=1.0 / 6.0, bias=0.5
+                    )
+                    ramps[(chunk, pair)] = ramp
 
             def multiply_side(chunk, pair, side):
                 if pair == 0 and side == 0:
@@ -198,22 +187,25 @@ def tile_attention_pb_t_kernel(tc, h_attn, proj_w, proj_g, proj_b, out):
                         name="grouped",
                         align_bytes=64,
                     )
+                blocks, values = by_side(chunk, pair)
                 nc.vector.scalar_tensor_tensor(
-                    out=grouped[chunk][:, pair * PAIR : (pair + 1) * PAIR, side],
-                    in0=ramps[(chunk, pair)][:, side].rearrange("q (s m) e -> q s m e", s=PAIR),
+                    out=grouped[chunk][:, pair * PAIR : pair * PAIR + blocks, side],
+                    in0=ramps[(chunk, pair)][:, side].rearrange("q (s m) e -> q s m e", s=blocks),
                     scalar=1.0,
-                    in1=by_side(chunk, pair)[:, side].rearrange("q (s m) e -> q s m e", s=PAIR),
+                    in1=values[:, side].rearrange("q (s m) e -> q s m e", s=blocks),
                     op0=ALU.min,
                     op1=ALU.mult,
                 )
 
-            def take_rows(chunk, pair):
+            def take_rows(chunk):
                 nc.vector.tensor_copy(
-                    out=grouped[chunk][:, pair * PAIR : (pair + 1) * PAIR]
-                    .rearrange("q b r m e -> q (b r m e)")
+                    out=grouped[chunk][:, CHUNK_BLOCKS[chunk] - 1]
+                    .rearrange("q r m e -> q (r m e)")
                     .bitcast(F32)
-                    .rearrange("q (c u) -> q c u", u=WORDS),
-                    in_=xT_banks[(chunk, pair)][:].rearrange("q u c -> q c u"),
+                    .rearrange("q (r j u) -> q r j u", r=SIDES, u=WORDS),
+                    in_=xT_banks[(chunk, pairs[chunk] - 1)][:, PAIR - 1].rearrange(
+                        "q j u r -> q r j u"
+                    ),
                 )
 
             def quantise(chunk):
@@ -293,18 +285,19 @@ def tile_attention_pb_t_kernel(tc, h_attn, proj_w, proj_g, proj_b, out):
                     make_ramps(step)
                     multiply_side(step, 0, 0)
                 if 1 <= step <= CHUNKS:
-                    if step - 1 in GP_BLOCKS:
-                        swish_rows(*GP_BLOCKS[step - 1])
+                    if GP_FIRST < step + GP_LEAD < CHUNKS:
+                        swish_rows(step + GP_LEAD)
                     quantise(step - 1)
                     products(step - 1)
                 if step < CHUNKS:
                     multiply_side(step, 0, 1)
                     if pairs[step] > 1:
-                        if (step, 1) in h_rows:
-                            take_rows(step, 1)
-                        else:
-                            multiply_side(step, 1, 0)
-                            multiply_side(step, 1, 1)
+                        multiply_side(step, 1, 0)
+                        multiply_side(step, 1, 1)
+                    if step >= GP_FIRST:
+                        take_rows(step)
+                if step == 0:
+                    swish_rows(GP_FIRST)
                 if step == 1:
                     choose_pivot()
                 if step >= 2:

@@ -23,7 +23,7 @@ PAIR = 2
 CHUNK_BLOCKS = [2] + [4] * 15 + [2]
 CHUNKS = len(CHUNK_BLOCKS)
 MAX_CHUNK = max(CHUNK_BLOCKS) * P
-GP_LEAD = 3
+GP_LEAD = 4
 GP_FIRST = GP_LEAD
 SUM_WIDTH = PAIR * P
 EPS = 1e-5
@@ -140,23 +140,39 @@ def tile_attention_pb_t_kernel(tc, h_attn, proj_w, proj_g, proj_b, out):
                             )
                     xT_banks[(chunk, pair)] = xT
 
-            def swish_rows(chunk):
-                v = x_tiles[chunk][:, CHUNK_BLOCKS[chunk] - 1, :]
+            ramp_rows = {}
+
+            def last_block(chunk):
+                return x_tiles[chunk][:, CHUNK_BLOCKS[chunk] - 1, :]
+
+            def make_ramp_rows(chunk):
                 clipped = stage.tile([P, K], BF16)
                 nc.vector.tensor_scalar(
-                    out=clipped[:], in0=v, scalar1=-3.0, scalar2=3.0, op0=ALU.max, op1=ALU.min
+                    out=clipped[:],
+                    in0=last_block(chunk),
+                    scalar1=-3.0,
+                    scalar2=3.0,
+                    op0=ALU.max,
+                    op1=ALU.min,
                 )
-                ramp_rows = stage.tile([P, K], F32)
+                ramp_rows[chunk] = stage.tile([P, K], F32, name="ramp_rows")
                 nc.gpsimd.tensor_scalar(
-                    out=ramp_rows[:],
+                    out=ramp_rows[chunk][:],
                     in0=clipped[:],
                     scalar1=3.0,
                     scalar2=1.0 / 6.0,
                     op0=ALU.add,
                     op1=ALU.mult,
                 )
+
+            def multiply_rows(chunk):
                 h_rows[chunk] = stage.tile([P, K], BF16, name="h_block")
-                nc.gpsimd.tensor_tensor(out=h_rows[chunk][:], in0=ramp_rows[:], in1=v, op=ALU.mult)
+                nc.gpsimd.tensor_tensor(
+                    out=h_rows[chunk][:],
+                    in0=ramp_rows[chunk][:],
+                    in1=last_block(chunk),
+                    op=ALU.mult,
+                )
 
             ramps = {}
             grouped = {}
@@ -285,8 +301,12 @@ def tile_attention_pb_t_kernel(tc, h_attn, proj_w, proj_g, proj_b, out):
                     make_ramps(step)
                     multiply_side(step, 0, 0)
                 if 1 <= step <= CHUNKS:
+                    if step == 1:
+                        make_ramp_rows(GP_FIRST)
                     if GP_FIRST < step + GP_LEAD < CHUNKS:
-                        swish_rows(step + GP_LEAD)
+                        make_ramp_rows(step + GP_LEAD)
+                    if GP_FIRST <= step - 1 + GP_LEAD < CHUNKS:
+                        multiply_rows(step - 1 + GP_LEAD)
                     quantise(step - 1)
                     products(step - 1)
                 if step < CHUNKS:
@@ -296,8 +316,6 @@ def tile_attention_pb_t_kernel(tc, h_attn, proj_w, proj_g, proj_b, out):
                         multiply_side(step, 1, 1)
                     if step >= GP_FIRST:
                         take_rows(step)
-                if step == 0:
-                    swish_rows(GP_FIRST)
                 if step == 1:
                     choose_pivot()
                 if step >= 2:
@@ -323,6 +341,10 @@ def tile_attention_pb_t_kernel(tc, h_attn, proj_w, proj_g, proj_b, out):
                 )
             neg_mean = keep.tile([P, HALVES], F32)
             nc.vector.tensor_scalar_mul(neg_mean[:], total[:], -1.0 / ROWS)
+            neg_mean_g = keep.tile([P, HALVES], F32)
+            nc.vector.tensor_tensor(
+                out=neg_mean_g[:], in0=neg_mean[:], in1=gb[:, 0:HALVES], op=ALU.mult
+            )
 
             def each_half(result, **args):
                 for half in range(HALVES):
@@ -369,8 +391,8 @@ def tile_attention_pb_t_kernel(tc, h_attn, proj_w, proj_g, proj_b, out):
             each_half(
                 shift,
                 func=ACT.Identity,
-                in_=neg_mean,
-                scale=lambda c: gain[:, c],
+                in_=neg_mean_g,
+                scale=lambda c: rstd[:, c],
                 bias=lambda c: gb[:, slice(HALVES + c.start, HALVES + c.stop)],
             )
 
@@ -384,8 +406,9 @@ def tile_attention_pb_t_kernel(tc, h_attn, proj_w, proj_g, proj_b, out):
             rows_gs = keep.tile([P, 2, P], F32)
             last_half = HALVES - 1
 
+            spread = psum_o.tile([P, 2, P], F32, tag="oT", name="spread")
+
             def spread_gain_and_shift():
-                spread = psum_o.tile([P, 2, P], F32, tag="oT", name="spread")
                 for which, numbers in enumerate((gain, shift)):
                     nc.tensor.matmul(
                         spread[:, which, :],
@@ -394,7 +417,6 @@ def tile_attention_pb_t_kernel(tc, h_attn, proj_w, proj_g, proj_b, out):
                         start=True,
                         stop=True,
                     )
-                nc.vector.tensor_copy(out=rows_gs[:], in_=spread[:])
 
             def products_again(chunk):
                 blocks = CHUNK_BLOCKS[chunk]
@@ -452,7 +474,7 @@ def tile_attention_pb_t_kernel(tc, h_attn, proj_w, proj_g, proj_b, out):
                     in1=rows_gs[:, 0:1, :].to_broadcast([P, blocks, P]),
                     op=ALU.mult,
                 )
-                engine = nc.vector if chunk % 3 == 1 else nc.gpsimd
+                engine = nc.vector if chunk < 3 or chunk % 3 == 1 else nc.gpsimd
                 engine.tensor_tensor(
                     out=results[chunk][:, :, last_half * P : HALVES * P],
                     in0=scaled[:],
@@ -476,13 +498,13 @@ def tile_attention_pb_t_kernel(tc, h_attn, proj_w, proj_g, proj_b, out):
 
             products_again(0)
             products_again(1)
+            spread_gain_and_shift()
             normalise(0)
+            nc.vector.tensor_copy(out=rows_gs[:], in_=spread[:])
             for chunk in range(CHUNKS):
                 if chunk + 1 < CHUNKS:
                     normalise(chunk + 1)
                 transpose_back_and_store(chunk)
-                if chunk == 0:
-                    spread_gain_and_shift()
                 if chunk + 1 < CHUNKS:
                     normalise_rows(chunk + 1)
                 if chunk + 2 < CHUNKS:

@@ -23,8 +23,9 @@ PAIR = 2
 CHUNK_BLOCKS = [2] + [4] * 15 + [2]
 CHUNKS = len(CHUNK_BLOCKS)
 MAX_CHUNK = max(CHUNK_BLOCKS) * P
+GP_FIRST = 3
+GP_STEPPED = 2
 GP_LEAD = 4
-GP_FIRST = GP_LEAD
 SUM_WIDTH = PAIR * P
 EPS = 1e-5
 
@@ -189,7 +190,7 @@ def tile_attention_pb_t_kernel(tc, h_attn, proj_w, proj_g, proj_b, out):
             def make_ramps(chunk):
                 for pair in range(pairs[chunk]):
                     blocks, values = by_side(chunk, pair)
-                    ramp = stage.tile([P, SIDES, blocks * SIDE * WORDS, 2], F32, name="ramp")
+                    ramp = stage.tile([P, SIDES, blocks * SIDE * WORDS, 2], F32, name="ramp", bufs=4)
                     nc.scalar.activation(
                         out=ramp[:], in_=values, func=ACT.Relu, scale=1.0 / 6.0, bias=0.5
                     )
@@ -295,18 +296,17 @@ def tile_attention_pb_t_kernel(tc, h_attn, proj_w, proj_g, proj_b, out):
             transposes(1)
             gbT = psum_y.tile([P, P], BF16, tag="y")
             nc.tensor.transpose(gbT[:], gb_rows[:], ident_bf16[:])
-            nc.vector.tensor_copy(out=gb[:], in_=gbT[:, 0 : 2 * HALVES])
             for step in range(CHUNKS + 2):
                 if step < CHUNKS:
                     make_ramps(step)
                     multiply_side(step, 0, 0)
                 if 1 <= step <= CHUNKS:
-                    if step == 1:
-                        make_ramp_rows(GP_FIRST)
-                    if GP_FIRST < step + GP_LEAD < CHUNKS:
+                    if step <= GP_STEPPED:
+                        make_ramp_rows(step + GP_FIRST)
+                    if GP_STEPPED <= step < CHUNKS - GP_LEAD:
                         make_ramp_rows(step + GP_LEAD)
-                    if GP_FIRST <= step - 1 + GP_LEAD < CHUNKS:
-                        multiply_rows(step - 1 + GP_LEAD)
+                    if step < CHUNKS - GP_FIRST:
+                        multiply_rows(step + GP_FIRST)
                     quantise(step - 1)
                     products(step - 1)
                 if step < CHUNKS:
@@ -316,6 +316,10 @@ def tile_attention_pb_t_kernel(tc, h_attn, proj_w, proj_g, proj_b, out):
                         multiply_side(step, 1, 1)
                     if step >= GP_FIRST:
                         take_rows(step)
+                if step == 0:
+                    make_ramp_rows(GP_FIRST)
+                    multiply_rows(GP_FIRST)
+                    nc.vector.tensor_copy(out=gb[:], in_=gbT[:, 0 : 2 * HALVES])
                 if step == 1:
                     choose_pivot()
                 if step >= 2:

@@ -20,13 +20,12 @@ ROWS = 32 * 256
 FEATURES = 256
 HALVES = FEATURES // P
 PAIR = 2
-CHUNK_BLOCKS = [2] + [4] * 15 + [2]
+CHUNK_BLOCKS = [1, 2] + [4] * 15 + [1]
 CHUNKS = len(CHUNK_BLOCKS)
-MAX_CHUNK = max(CHUNK_BLOCKS) * P
-GP_FIRST = 3
-GP_STEPPED = 2
-GP_LEAD = 4
-SUM_WIDTH = PAIR * P
+FULL = 4 * P
+DRAIN = CHUNKS - 2
+GP_FIRST = 4
+GP_LEAD = 2
 EPS = 1e-5
 
 FLOPS = 2 * ROWS * K * FEATURES
@@ -45,7 +44,7 @@ def tile_attention_pb_t_kernel(tc, h_attn, proj_w, proj_g, proj_b, out):
     out_chunks = [
         out_all[cols[i], :].rearrange("(p j) c -> p j c", j=CHUNK_BLOCKS[i]) for i in range(CHUNKS)
     ]
-    pairs = [CHUNK_BLOCKS[i] // PAIR for i in range(CHUNKS)]
+    pairs = [-(-CHUNK_BLOCKS[i] // PAIR) for i in range(CHUNKS)]
 
     with tc.manual_schedule(), tc.tile_pool(name="keep", bufs=1) as keep, tc.tile_pool(
         name="stage", bufs=3
@@ -57,10 +56,10 @@ def tile_attention_pb_t_kernel(tc, h_attn, proj_w, proj_g, proj_b, out):
             nc.sync.dma_start(out=x_rows[:], in_=x_chunks[chunk])
             x_tiles.append(x_rows)
 
-        load(0)
+        for chunk in range(3):
+            load(chunk)
         w_rows = keep.tile([P, HALVES, K], BF16)
         nc.sync.dma_start(out=w_rows[:], in_=proj_w.rearrange("(h c) k -> c h k", h=HALVES))
-        load(1)
         gb_rows = keep.tile([P, P], BF16)
         nc.vector.memset(gb_rows[:], 0.0)
         nc.sync.dma_start(
@@ -69,7 +68,7 @@ def tile_attention_pb_t_kernel(tc, h_attn, proj_w, proj_g, proj_b, out):
         nc.sync.dma_start(
             out=gb_rows[HALVES : 2 * HALVES, :], in_=proj_b.rearrange("(h c) -> h c", h=HALVES)
         )
-        for chunk in range(2, CHUNKS):
+        for chunk in range(3, CHUNKS):
             load(chunk)
 
         ident_f32 = keep.tile([P, P], F32)
@@ -103,9 +102,8 @@ def tile_attention_pb_t_kernel(tc, h_attn, proj_w, proj_g, proj_b, out):
             )
 
         gb = keep.tile([P, 2 * HALVES], F32)
-        neg_pivot = keep.tile([P, HALVES], F32)
         pivot = keep.tile([P, HALVES], F32)
-        sq_parts = keep.tile([P, HALVES, CHUNKS - 1], F32)
+        sq_parts = keep.tile([P, HALVES, CHUNKS - 2], F32)
         sq_last = keep.tile([P, HALVES], F32)
         gain = keep.tile([P, HALVES], F32)
         shift = keep.tile([P, HALVES], F32)
@@ -114,28 +112,29 @@ def tile_attention_pb_t_kernel(tc, h_attn, proj_w, proj_g, proj_b, out):
             name="psum_y", bufs=2
         ) as psum_y, tc.psum_pool(name="psum_sum", bufs=1) as psum_sum:
             row_sums = [
-                psum_sum.tile([P, SUM_WIDTH], F32, name="row_sums%d" % half)
-                for half in range(HALVES)
+                psum_sum.tile([P, P], F32, name="row_sums%d" % half) for half in range(HALVES)
             ]
             xT_banks = {}
             h_rows = {}
             y_banks = {}
 
             def by_gpsimd(chunk, block):
-                return chunk >= GP_FIRST and block == CHUNK_BLOCKS[chunk] - 1
+                return GP_FIRST <= chunk < CHUNKS - 1 and block == CHUNK_BLOCKS[chunk] - 1
+
+            def pair_blocks(chunk, pair):
+                return range(pair * PAIR, min((pair + 1) * PAIR, CHUNK_BLOCKS[chunk]))
 
             def transposes(chunk):
                 for pair in range(pairs[chunk]):
                     xT = psum_t.tile([P, PAIR, SIDE, WORDS, SIDES], F32, tag="xT", name="xT")
-                    for s in range(PAIR):
-                        block = pair * PAIR + s
+                    for block in pair_blocks(chunk, pair):
                         if by_gpsimd(chunk, block):
                             words = h_rows[chunk][:].bitcast(F32)
                         else:
                             words = x_tiles[chunk][:, block, :].bitcast(F32)
                         for u in range(WORDS):
                             nc.tensor.transpose(
-                                xT[:, s, :, u, :],
+                                xT[:, block - pair * PAIR, :, u, :],
                                 words[:, u : K // 2 : WORDS],
                                 ident_sides[:],
                             )
@@ -179,7 +178,7 @@ def tile_attention_pb_t_kernel(tc, h_attn, proj_w, proj_g, proj_b, out):
             grouped = {}
 
             def by_side(chunk, pair):
-                blocks = PAIR - by_gpsimd(chunk, (pair + 1) * PAIR - 1)
+                blocks = len([b for b in pair_blocks(chunk, pair) if not by_gpsimd(chunk, b)])
                 return blocks, (
                     xT_banks[(chunk, pair)][:, 0:blocks]
                     .rearrange("q s j u r -> q (s j u r)")
@@ -232,103 +231,140 @@ def tile_attention_pb_t_kernel(tc, h_attn, proj_w, proj_g, proj_b, out):
                     in_=grouped[chunk][:].rearrange("q b r m e -> q (b r m e)"),
                 )
 
-            def products(chunk):
+            def products(*chunks):
+                start = starts[chunks[0]]
+                rows = P * sum(CHUNK_BLOCKS[chunk] for chunk in chunks)
                 for half in range(HALVES):
-                    y = psum_y.tile([P, CHUNK_BLOCKS[chunk] * P], F32, name="y")
-                    multiply(y[:], half, cols[chunk], True, True)
-                    y_banks[(chunk, half)] = y
-                    for pair in range(pairs[chunk]):
-                        first = starts[chunk] + pair * SUM_WIDTH
+                    if chunks[0] < DRAIN:
+                        y = psum_y.tile([P, rows], F32, tag="y", name="y")
+                    else:
+                        y = psum_t.tile([P, rows], F32, tag="xT", name="y")
+                    y_banks[(chunks[0], half)] = y
+                    for chunk in chunks:
+                        first = starts[chunk] - start
+                        multiply(
+                            y[:, first : first + P * CHUNK_BLOCKS[chunk]], half, cols[chunk], True, True
+                        )
+                    for first in range(start, start + rows, P):
                         multiply(
                             row_sums[half][:],
                             half,
-                            slice(first, first + SUM_WIDTH),
+                            slice(first, first + P),
                             first == 0,
-                            first == ROWS - SUM_WIDTH,
+                            first == ROWS - P,
                         )
 
             def choose_pivot():
-                first_sum = keep.tile([P, HALVES], F32)
                 for half in range(HALVES):
-                    nc.vector.tensor_reduce(
-                        out=first_sum[:, half : half + 1],
+                    unread = stage.tile([P, FULL], BF16, name="unread")
+                    nc.scalar.activation(
+                        out=unread[:, 0:P],
                         in_=y_banks[(0, half)][:, 0:P],
-                        axis=X_AXIS,
-                        op=ALU.add,
+                        func=ACT.Identity,
+                        scale=1.0 / P,
+                        accum_out=pivot[:, half : half + 1],
                     )
-                nc.vector.tensor_scalar_mul(neg_pivot[:], first_sum[:], -1.0 / P)
-                nc.vector.tensor_scalar_mul(pivot[:], first_sum[:], 1.0 / P)
 
             def squares(chunk):
                 for half in range(HALVES):
-                    unread = stage.tile([P, MAX_CHUNK], BF16)
+                    y = y_banks[(chunk, half)]
+                    unread = stage.tile([P, FULL], BF16, name="unread")
                     if chunk < CHUNKS - 1:
-                        sum_of_squares = sq_parts[:, half, chunk : chunk + 1]
+                        column = max(chunk - 1, 0)
+                        sum_of_squares = sq_parts[:, half, column : column + 1]
                     else:
                         sum_of_squares = sq_last[:, half : half + 1]
                     nc.scalar.activation(
-                        out=unread[:, 0 : CHUNK_BLOCKS[chunk] * P],
-                        in_=y_banks[(chunk, half)][:],
+                        out=unread[:, 0 : y.shape[1]],
+                        in_=y[:],
                         func=ACT.Square,
-                        bias=neg_pivot[:, half : half + 1],
+                        scale=-1.0,
+                        bias=pivot[:, half : half + 1],
                         accum_out=sum_of_squares,
                     )
 
-            transposes(0)
-
-            wT = psum_y.tile([P, WORDS, FEATURES], F32, tag="y")
-            for half in range(HALVES):
-                words = w_rows[:, half, :].bitcast(F32)
-                for u in range(WORDS):
-                    nc.tensor.transpose(
-                        wT[:, u, half * P : (half + 1) * P],
-                        words[:, u : K // 2 : WORDS],
-                        ident_f32[:],
-                    )
+            wT = psum_y.tile([P, WORDS, FEATURES], F32, tag="y", name="wT")
+            gbT = psum_y.tile([P, P], BF16, tag="y", name="gbT")
             w_grouped = keep.tile([P, FEATURES * PACK], BF16, align_bytes=64)
-            nc.vector.tensor_copy(
-                out=w_grouped[:].bitcast(F32).rearrange("q (c u) -> q c u", u=WORDS),
-                in_=wT[:].rearrange("q u c -> q c u"),
-            )
-            nc.vector.quantize_mx(
-                out=w_codes[:].bitcast(FP8X4), scales=w_scales[:], in_=w_grouped[:]
-            )
+
+            def transpose_weights():
+                for half in range(HALVES):
+                    words = w_rows[:, half, :].bitcast(F32)
+                    for u in range(WORDS):
+                        nc.tensor.transpose(
+                            wT[:, u, half * P : (half + 1) * P],
+                            words[:, u : K // 2 : WORDS],
+                            ident_f32[:],
+                        )
+                nc.tensor.transpose(gbT[:], gb_rows[:], ident_bf16[:])
+
+            def group_weights():
+                nc.scalar.copy(
+                    out=w_grouped[:].bitcast(F32).rearrange("q (c u) -> q c u", u=WORDS),
+                    in_=wT[:].rearrange("q u c -> q c u"),
+                )
+                nc.scalar.copy(out=gb[:], in_=gbT[:, 0 : 2 * HALVES])
+
+            def quantise_weights():
+                nc.vector.quantize_mx(
+                    out=w_codes[:].bitcast(FP8X4), scales=w_scales[:], in_=w_grouped[:]
+                )
+
+            transposes(0)
             transposes(1)
-            gbT = psum_y.tile([P, P], BF16, tag="y")
-            nc.tensor.transpose(gbT[:], gb_rows[:], ident_bf16[:])
             for step in range(CHUNKS + 2):
                 if step < CHUNKS:
                     make_ramps(step)
                     multiply_side(step, 0, 0)
+                if step == 2:
+                    group_weights()
                 if 1 <= step <= CHUNKS:
-                    if step <= GP_STEPPED:
-                        make_ramp_rows(step + GP_FIRST)
-                    if GP_STEPPED <= step < CHUNKS - GP_LEAD:
-                        make_ramp_rows(step + GP_LEAD)
-                    if step < CHUNKS - GP_FIRST:
-                        multiply_rows(step + GP_FIRST)
+                    if GP_FIRST < step + GP_LEAD + 1 < CHUNKS - 1:
+                        make_ramp_rows(step + GP_LEAD + 1)
+                    if GP_FIRST <= step + GP_LEAD < CHUNKS - 1:
+                        multiply_rows(step + GP_LEAD)
                     quantise(step - 1)
-                    products(step - 1)
                 if step < CHUNKS:
                     multiply_side(step, 0, 1)
+                if step == 2:
+                    quantise_weights()
+                    products(0, 1)
+                if 2 < step <= CHUNKS:
+                    products(step - 1)
+                if step < CHUNKS:
                     if pairs[step] > 1:
                         multiply_side(step, 1, 0)
                         multiply_side(step, 1, 1)
-                    if step >= GP_FIRST:
+                    if by_gpsimd(step, CHUNK_BLOCKS[step] - 1):
                         take_rows(step)
-                if step == 0:
+                if step + GP_LEAD + 1 == GP_FIRST:
                     make_ramp_rows(GP_FIRST)
-                    multiply_rows(GP_FIRST)
-                    nc.vector.tensor_copy(out=gb[:], in_=gbT[:, 0 : 2 * HALVES])
-                if step == 1:
+                if step == 3:
                     choose_pivot()
-                if step >= 2:
+                    squares(0)
+                if step > 3:
                     squares(step - 2)
                 if step + 2 < CHUNKS:
                     transposes(step + 2)
+                if step == 0:
+                    transpose_weights()
 
+            total = keep.tile([P, HALVES], F32)
+            for half in range(HALVES):
+                nc.vector.tensor_reduce(
+                    out=total[:, half : half + 1], in_=row_sums[half][:], axis=X_AXIS, op=ALU.add
+                )
             sq_total = keep.tile([P, HALVES], F32)
             nc.vector.tensor_reduce(out=sq_total[:], in_=sq_parts[:], axis=X_AXIS, op=ALU.add)
+            neg_mean_g = keep.tile([P, HALVES], F32)
+            nc.vector.scalar_tensor_tensor(
+                out=neg_mean_g[:],
+                in0=total[:],
+                scalar=-1.0 / ROWS,
+                in1=gb[:, 0:HALVES],
+                op0=ALU.mult,
+                op1=ALU.mult,
+            )
             sq_mean = keep.tile([P, HALVES], F32)
             nc.vector.tensor_scalar(
                 out=sq_mean[:],
@@ -337,17 +373,6 @@ def tile_attention_pb_t_kernel(tc, h_attn, proj_w, proj_g, proj_b, out):
                 scalar2=EPS,
                 op0=ALU.mult,
                 op1=ALU.add,
-            )
-            total = keep.tile([P, HALVES], F32)
-            for half in range(HALVES):
-                nc.vector.tensor_reduce(
-                    out=total[:, half : half + 1], in_=row_sums[half][:], axis=X_AXIS, op=ALU.add
-                )
-            neg_mean = keep.tile([P, HALVES], F32)
-            nc.vector.tensor_scalar_mul(neg_mean[:], total[:], -1.0 / ROWS)
-            neg_mean_g = keep.tile([P, HALVES], F32)
-            nc.vector.tensor_tensor(
-                out=neg_mean_g[:], in0=neg_mean[:], in1=gb[:, 0:HALVES], op=ALU.mult
             )
 
             def each_half(result, **args):
@@ -361,14 +386,6 @@ def tile_attention_pb_t_kernel(tc, h_attn, proj_w, proj_g, proj_b, out):
                         bias=args["bias"](column),
                     )
 
-            sq_eps = keep.tile([P, HALVES], F32)
-            each_half(
-                sq_eps,
-                func=ACT.Identity,
-                in_=sq_last,
-                scale=lambda c: 1.0 / ROWS,
-                bias=lambda c: sq_mean[:, c],
-            )
             off_sq = keep.tile([P, HALVES], F32)
             each_half(
                 off_sq,
@@ -376,6 +393,14 @@ def tile_attention_pb_t_kernel(tc, h_attn, proj_w, proj_g, proj_b, out):
                 in_=total,
                 scale=lambda c: -1.0 / ROWS,
                 bias=lambda c: pivot[:, c],
+            )
+            sq_eps = keep.tile([P, HALVES], F32)
+            each_half(
+                sq_eps,
+                func=ACT.Identity,
+                in_=sq_last,
+                scale=lambda c: 1.0 / ROWS,
+                bias=lambda c: sq_mean[:, c],
             )
             rstd = keep.tile([P, HALVES], F32)
             each_half(
@@ -385,13 +410,7 @@ def tile_attention_pb_t_kernel(tc, h_attn, proj_w, proj_g, proj_b, out):
                 scale=lambda c: -1.0,
                 bias=lambda c: sq_eps[:, c],
             )
-            each_half(
-                gain,
-                func=ACT.Identity,
-                in_=gb,
-                scale=lambda c: rstd[:, c],
-                bias=lambda c: 0.0,
-            )
+            nc.vector.tensor_tensor(out=gain[:], in0=rstd[:], in1=gb[:, 0:HALVES], op=ALU.mult)
             each_half(
                 shift,
                 func=ACT.Identity,
@@ -400,68 +419,79 @@ def tile_attention_pb_t_kernel(tc, h_attn, proj_w, proj_g, proj_b, out):
                 bias=lambda c: gb[:, slice(HALVES + c.start, HALVES + c.stop)],
             )
 
-        with tc.psum_pool(name="psum_y2", bufs=3, reuse_waits="tile") as psum_y2, tc.psum_pool(
-            name="psum_o", bufs=2, reuse_waits="tile"
-        ) as psum_o, tc.psum_pool(name="psum_r", bufs=3, reuse_waits="tile") as psum_r:
+        with tc.psum_pool(name="psum_o", bufs=3, reuse_waits="tile") as psum_o, tc.psum_pool(
+            name="psum_s", bufs=1, reuse_waits="tile"
+        ) as psum_s, tc.psum_pool(name="psum_y2", bufs=2, reuse_waits="tile") as psum_y2, tc.psum_pool(
+            name="psum_r", bufs=2, reuse_waits="tile"
+        ) as psum_r:
             y2_banks = {}
             yR_banks = {}
             normed = {}
+            scaled_rows = {}
+            oT_banks = {}
             results = {}
             rows_gs = keep.tile([P, 2, P], F32)
             last_half = HALVES - 1
+            last_features = slice(last_half * P, HALVES * P)
 
-            spread = psum_o.tile([P, 2, P], F32, tag="oT", name="spread")
+            def halves_by_features(chunk):
+                return HALVES if chunk < 2 else 1
 
-            def spread_gain_and_shift():
-                for which, numbers in enumerate((gain, shift)):
-                    nc.tensor.matmul(
-                        spread[:, which, :],
-                        lhsT=numbers[:, last_half:HALVES].to_broadcast([P, P]),
-                        rhs=ident_f32[:],
+            def products_by_features(chunk):
+                rows = P * CHUNK_BLOCKS[chunk]
+                if chunk == 1:
+                    banks = [psum_r.tile([P, rows], F32, tag="yR", name="y2") for half in range(HALVES)]
+                    parts = [bank[:] for bank in banks]
+                else:
+                    bank = psum_y2.tile([P, halves_by_features(chunk), rows], F32, tag="y2", name="y2")
+                    parts = [bank[:, half, :] for half in range(halves_by_features(chunk))]
+                for half in range(len(parts)):
+                    multiply(parts[half], half, cols[chunk], True, True)
+                    y2_banks[(chunk, half)] = parts[half]
+
+            def products_by_rows(chunk):
+                yR = psum_r.tile([P, CHUNK_BLOCKS[chunk], P], F32, tag="yR", name="yR")
+                for block in range(CHUNK_BLOCKS[chunk]):
+                    rows = slice(starts[chunk] + block * P, starts[chunk] + (block + 1) * P)
+                    nc.tensor.matmul_mx(
+                        out=yR[:, block, :],
+                        lhsT=h_codes[:, rows].bitcast(FP8X4),
+                        lhsT_scale=h_scales[:, rows],
+                        rhs=w_codes[:, last_features].bitcast(FP8X4),
+                        rhs_scale=w_scales[:, last_features],
                         start=True,
                         stop=True,
                     )
+                yR_banks[chunk] = yR
 
-            def products_again(chunk):
-                blocks = CHUNK_BLOCKS[chunk]
-                for half in range(HALVES if chunk == 0 else 1):
-                    y2 = psum_y2.tile([P, blocks * P], F32, name="y2")
-                    multiply(y2[:], half, cols[chunk], True, True)
-                    y2_banks[(chunk, half)] = y2
-                if chunk > 0:
-                    yR = psum_r.tile([P, blocks, P], F32, name="yR")
-                    features = slice(last_half * P, HALVES * P)
-                    for block in range(blocks):
-                        rows = slice(starts[chunk] + block * P, starts[chunk] + (block + 1) * P)
-                        nc.tensor.matmul_mx(
-                            out=yR[:, block, :],
-                            lhsT=h_codes[:, rows].bitcast(FP8X4),
-                            lhsT_scale=h_scales[:, rows],
-                            rhs=w_codes[:, features].bitcast(FP8X4),
-                            rhs_scale=w_scales[:, features],
-                            start=True,
-                            stop=True,
-                        )
-                    yR_banks[chunk] = yR
+            def spread_gain_and_shift():
+                spread = psum_s.tile([P, 2, P], F32, name="spread")
+                for which, numbers in enumerate((gain, shift)):
+                    nc.tensor.transpose(
+                        spread[:, which, :],
+                        numbers[:, last_half:HALVES].to_broadcast([P, P]),
+                        ident_f32[:],
+                    )
+                return spread
 
             def normalise(chunk):
                 blocks = CHUNK_BLOCKS[chunk]
-                results[chunk] = stage.tile([P, blocks, FEATURES], F32, name="result", bufs=6)
-                for half in range(HALVES if chunk == 0 else 1):
+                results[chunk] = stage.tile([P, blocks, FEATURES], F32, name="result", bufs=8)
+                for half in range(halves_by_features(chunk)):
                     column = slice(half, half + 1)
-                    normed_half = stage.tile([P, MAX_CHUNK], F32, name="normed%d" % half)
+                    normed_half = stage.tile([P, blocks * P], F32, name="normed%d" % half)
                     if half == 0:
                         nc.scalar.activation(
-                            out=normed_half[:, 0 : blocks * P],
-                            in_=y2_banks[(chunk, half)][:],
+                            out=normed_half[:],
+                            in_=y2_banks[(chunk, half)],
                             func=ACT.Identity,
                             scale=gain[:, column],
                             bias=shift[:, column],
                         )
                     else:
                         nc.vector.tensor_scalar(
-                            out=normed_half[:, 0 : blocks * P],
-                            in0=y2_banks[(chunk, half)][:],
+                            out=normed_half[:],
+                            in0=y2_banks[(chunk, half)],
                             scalar1=gain[:, column],
                             scalar2=shift[:, column],
                             op0=ALU.mult,
@@ -469,47 +499,76 @@ def tile_attention_pb_t_kernel(tc, h_attn, proj_w, proj_g, proj_b, out):
                         )
                     normed[(chunk, half)] = normed_half
 
-            def normalise_rows(chunk):
+            def scale_rows(chunk):
                 blocks = CHUNK_BLOCKS[chunk]
-                scaled = stage.tile([P, blocks, P], F32, name="scaled")
+                scaled_rows[chunk] = stage.tile([P, blocks, P], F32, name="scaled")
                 nc.vector.tensor_tensor(
-                    out=scaled[:],
+                    out=scaled_rows[chunk][:],
                     in0=yR_banks[chunk][:],
                     in1=rows_gs[:, 0:1, :].to_broadcast([P, blocks, P]),
                     op=ALU.mult,
                 )
-                engine = nc.vector if chunk < 3 or chunk % 3 == 1 else nc.gpsimd
+
+            def shift_rows(chunk):
+                engine, shifts = (nc.vector, spread) if chunk % 3 == 1 else (nc.gpsimd, rows_gs)
                 engine.tensor_tensor(
-                    out=results[chunk][:, :, last_half * P : HALVES * P],
-                    in0=scaled[:],
-                    in1=rows_gs[:, 1:2, :].to_broadcast([P, blocks, P]),
+                    out=results[chunk][:, :, last_features],
+                    in0=scaled_rows[chunk][:],
+                    in1=shifts[:, 1:2, :].to_broadcast([P, CHUNK_BLOCKS[chunk], P]),
                     op=ALU.add,
                 )
 
-            def transpose_back_and_store(chunk):
+            def transpose_back(chunk):
                 blocks = CHUNK_BLOCKS[chunk]
-                halves = HALVES if chunk == 0 else 1
-                oT = psum_o.tile([P, blocks, halves * P], F32, tag="oT", name="oT")
-                for block in range(blocks):
-                    for half in range(halves):
+                for half in range(halves_by_features(chunk)):
+                    if chunk > 0 or half == 0:
+                        oT = psum_o.tile([P, max(blocks, HALVES), P], F32, tag="oT", name="oT")
+                    for block in range(blocks):
                         nc.tensor.transpose(
-                            oT[:, block, half * P : (half + 1) * P],
+                            oT[:, half if chunk == 0 else block, :],
                             normed[(chunk, half)][:, block * P : (block + 1) * P],
                             ident_f32[:],
                         )
-                nc.scalar.copy(out=results[chunk][:, :, 0 : halves * P], in_=oT[:])
+                    oT_banks[(chunk, half)] = oT
+
+            def empty_and_store(chunk):
+                blocks = CHUNK_BLOCKS[chunk]
+                if chunk == 0:
+                    nc.scalar.copy(
+                        out=results[0][:].rearrange("p j (h c) -> p (j h) c", h=HALVES),
+                        in_=oT_banks[(0, 0)][:],
+                    )
+                else:
+                    for half in range(halves_by_features(chunk)):
+                        by_vector = half == last_half or (chunk > 2 and chunk % 3 == 2)
+                        copy = nc.vector.tensor_copy if by_vector else nc.scalar.copy
+                        copy(
+                            out=results[chunk][:, :, half * P : (half + 1) * P],
+                            in_=oT_banks[(chunk, half)][:, 0:blocks, :],
+                        )
+                if chunk + 1 < CHUNKS and chunk > 0:
+                    shift_rows(chunk + 1)
                 nc.sync.dma_start(out=out_chunks[chunk], in_=results[chunk][:])
 
-            products_again(0)
-            products_again(1)
-            spread_gain_and_shift()
+            products_by_features(0)
+            products_by_features(1)
+            products_by_features(2)
+            spread = spread_gain_and_shift()
             normalise(0)
+            normalise(1)
             nc.vector.tensor_copy(out=rows_gs[:], in_=spread[:])
+            products_by_rows(2)
+            transpose_back(0)
+            transpose_back(1)
+            normalise(2)
             for chunk in range(CHUNKS):
-                if chunk + 1 < CHUNKS:
-                    normalise(chunk + 1)
-                transpose_back_and_store(chunk)
-                if chunk + 1 < CHUNKS:
-                    normalise_rows(chunk + 1)
-                if chunk + 2 < CHUNKS:
-                    products_again(chunk + 2)
+                if chunk > 0 and chunk + 1 < CHUNKS:
+                    if chunk > 1:
+                        normalise(chunk + 1)
+                    scale_rows(chunk + 1)
+                if chunk > 1:
+                    transpose_back(chunk)
+                if chunk > 0 and chunk + 2 < CHUNKS:
+                    products_by_features(chunk + 2)
+                    products_by_rows(chunk + 2)
+                empty_and_store(chunk)

@@ -20,12 +20,14 @@ ROWS = 32 * 256
 FEATURES = 256
 HALVES = FEATURES // P
 PAIR = 2
-CHUNK_BLOCKS = [1, 2] + [4] * 15 + [1]
+CHUNK_BLOCKS = [1, 2] + [4] * 14 + [2, 2, 1]
 CHUNKS = len(CHUNK_BLOCKS)
 FULL = 4 * P
-DRAIN = CHUNKS - 2
+DRAIN = CHUNKS - 3
 GP_FIRST = 4
 GP_LEAD = 2
+PAIRS_FROM = 4
+WARM_PASSES = 5
 EPS = 1e-5
 
 FLOPS = 2 * ROWS * K * FEATURES
@@ -119,7 +121,7 @@ def tile_attention_pb_t_kernel(tc, h_attn, proj_w, proj_g, proj_b, out):
             y_banks = {}
 
             def by_gpsimd(chunk, block):
-                return GP_FIRST <= chunk < CHUNKS - 1 and block == CHUNK_BLOCKS[chunk] - 1
+                return GP_FIRST <= chunk and block == CHUNK_BLOCKS[chunk] - 1
 
             def pair_blocks(chunk, pair):
                 return range(pair * PAIR, min((pair + 1) * PAIR, CHUNK_BLOCKS[chunk]))
@@ -177,10 +179,12 @@ def tile_attention_pb_t_kernel(tc, h_attn, proj_w, proj_g, proj_b, out):
             ramps = {}
             grouped = {}
 
+            def side_blocks(chunk, pair):
+                return len([b for b in pair_blocks(chunk, pair) if not by_gpsimd(chunk, b)])
+
             def by_side(chunk, pair):
-                blocks = len([b for b in pair_blocks(chunk, pair) if not by_gpsimd(chunk, b)])
-                return blocks, (
-                    xT_banks[(chunk, pair)][:, 0:blocks]
+                return (
+                    xT_banks[(chunk, pair)][:, 0 : side_blocks(chunk, pair)]
                     .rearrange("q s j u r -> q (s j u r)")
                     .bitcast(BF16)
                     .rearrange("q (m r e) -> q r m e", r=SIDES, e=2)
@@ -188,10 +192,12 @@ def tile_attention_pb_t_kernel(tc, h_attn, proj_w, proj_g, proj_b, out):
 
             def make_ramps(chunk):
                 for pair in range(pairs[chunk]):
-                    blocks, values = by_side(chunk, pair)
+                    blocks = side_blocks(chunk, pair)
+                    if blocks == 0:
+                        continue
                     ramp = stage.tile([P, SIDES, blocks * SIDE * WORDS, 2], F32, name="ramp", bufs=4)
                     nc.scalar.activation(
-                        out=ramp[:], in_=values, func=ACT.Relu, scale=1.0 / 6.0, bias=0.5
+                        out=ramp[:], in_=by_side(chunk, pair), func=ACT.Relu, scale=1.0 / 6.0, bias=0.5
                     )
                     ramps[(chunk, pair)] = ramp
 
@@ -203,7 +209,10 @@ def tile_attention_pb_t_kernel(tc, h_attn, proj_w, proj_g, proj_b, out):
                         name="grouped",
                         align_bytes=64,
                     )
-                blocks, values = by_side(chunk, pair)
+                blocks = side_blocks(chunk, pair)
+                if blocks == 0:
+                    return
+                values = by_side(chunk, pair)
                 nc.vector.scalar_tensor_tensor(
                     out=grouped[chunk][:, pair * PAIR : pair * PAIR + blocks, side],
                     in0=ramps[(chunk, pair)][:, side].rearrange("q (s m) e -> q s m e", s=blocks),
@@ -214,12 +223,13 @@ def tile_attention_pb_t_kernel(tc, h_attn, proj_w, proj_g, proj_b, out):
                 )
 
             def take_rows(chunk):
+                last = CHUNK_BLOCKS[chunk] - 1
                 nc.vector.tensor_copy(
-                    out=grouped[chunk][:, CHUNK_BLOCKS[chunk] - 1]
+                    out=grouped[chunk][:, last]
                     .rearrange("q r m e -> q (r m e)")
                     .bitcast(F32)
                     .rearrange("q (r j u) -> q r j u", r=SIDES, u=WORDS),
-                    in_=xT_banks[(chunk, pairs[chunk] - 1)][:, PAIR - 1].rearrange(
+                    in_=xT_banks[(chunk, last // PAIR)][:, last % PAIR].rearrange(
                         "q j u r -> q r j u"
                     ),
                 )
@@ -316,12 +326,14 @@ def tile_attention_pb_t_kernel(tc, h_attn, proj_w, proj_g, proj_b, out):
                 if step < CHUNKS:
                     make_ramps(step)
                     multiply_side(step, 0, 0)
+                if step == CHUNKS - 1:
+                    take_rows(step)
                 if step == 2:
                     group_weights()
                 if 1 <= step <= CHUNKS:
-                    if GP_FIRST < step + GP_LEAD + 1 < CHUNKS - 1:
+                    if GP_FIRST < step + GP_LEAD + 1 < CHUNKS:
                         make_ramp_rows(step + GP_LEAD + 1)
-                    if GP_FIRST <= step + GP_LEAD < CHUNKS - 1:
+                    if GP_FIRST <= step + GP_LEAD < CHUNKS:
                         multiply_rows(step + GP_LEAD)
                     quantise(step - 1)
                 if step < CHUNKS:
@@ -335,7 +347,7 @@ def tile_attention_pb_t_kernel(tc, h_attn, proj_w, proj_g, proj_b, out):
                     if pairs[step] > 1:
                         multiply_side(step, 1, 0)
                         multiply_side(step, 1, 1)
-                    if by_gpsimd(step, CHUNK_BLOCKS[step] - 1):
+                    if GP_FIRST <= step < CHUNKS - 1:
                         take_rows(step)
                 if step + GP_LEAD + 1 == GP_FIRST:
                     make_ramp_rows(GP_FIRST)
@@ -476,10 +488,10 @@ def tile_attention_pb_t_kernel(tc, h_attn, proj_w, proj_g, proj_b, out):
 
             def normalise(chunk):
                 blocks = CHUNK_BLOCKS[chunk]
-                results[chunk] = stage.tile([P, blocks, FEATURES], F32, name="result", bufs=8)
+                results[chunk] = stage.tile([P, blocks, FEATURES], F32, name="result", bufs=10)
                 for half in range(halves_by_features(chunk)):
                     column = slice(half, half + 1)
-                    normed_half = stage.tile([P, blocks * P], F32, name="normed%d" % half)
+                    normed_half = stage.tile([P, blocks * P], F32, name="normed%d" % half, bufs=4)
                     if half == 0:
                         nc.scalar.activation(
                             out=normed_half[:],
@@ -501,7 +513,7 @@ def tile_attention_pb_t_kernel(tc, h_attn, proj_w, proj_g, proj_b, out):
 
             def scale_rows(chunk):
                 blocks = CHUNK_BLOCKS[chunk]
-                scaled_rows[chunk] = stage.tile([P, blocks, P], F32, name="scaled")
+                scaled_rows[chunk] = stage.tile([P, blocks, P], F32, name="scaled", bufs=4)
                 nc.vector.tensor_tensor(
                     out=scaled_rows[chunk][:],
                     in0=yR_banks[chunk][:],
@@ -553,6 +565,8 @@ def tile_attention_pb_t_kernel(tc, h_attn, proj_w, proj_g, proj_b, out):
             products_by_features(0)
             products_by_features(1)
             products_by_features(2)
+            for again in range(WARM_PASSES):
+                multiply(y2_banks[(2, 0)], 0, cols[2], True, True)
             spread = spread_gain_and_shift()
             normalise(0)
             normalise(1)
@@ -561,14 +575,30 @@ def tile_attention_pb_t_kernel(tc, h_attn, proj_w, proj_g, proj_b, out):
             transpose_back(0)
             transpose_back(1)
             normalise(2)
-            for chunk in range(CHUNKS):
-                if chunk > 0 and chunk + 1 < CHUNKS:
-                    if chunk > 1:
-                        normalise(chunk + 1)
+            for chunk in range(PAIRS_FROM - 1):
+                if chunk > 1:
+                    normalise(chunk + 1)
+                if chunk > 0:
                     scale_rows(chunk + 1)
                 if chunk > 1:
                     transpose_back(chunk)
-                if chunk > 0 and chunk + 2 < CHUNKS:
+                if chunk > 0:
                     products_by_features(chunk + 2)
                     products_by_rows(chunk + 2)
                 empty_and_store(chunk)
+            products_by_features(PAIRS_FROM + 1)
+            products_by_rows(PAIRS_FROM + 1)
+            for first in range(PAIRS_FROM, CHUNKS + 1, 2):
+                following = range(first + 2, min(first + 4, CHUNKS))
+                emptied = range(first - 1, min(first + 1, CHUNKS))
+                for chunk in range(first, min(first + 2, CHUNKS)):
+                    normalise(chunk)
+                    scale_rows(chunk)
+                for chunk in emptied:
+                    transpose_back(chunk)
+                for chunk in following:
+                    products_by_features(chunk)
+                for chunk in following:
+                    products_by_rows(chunk)
+                for chunk in emptied:
+                    empty_and_store(chunk)

@@ -20,14 +20,13 @@ ROWS = 32 * 256
 FEATURES = 256
 HALVES = FEATURES // P
 PAIR = 2
-CHUNK_BLOCKS = [1, 2] + [4] * 14 + [2, 2, 1]
+CHUNK_BLOCKS = [1, 2] + [4] * 15 + [1]
 CHUNKS = len(CHUNK_BLOCKS)
 FULL = 4 * P
-DRAIN = CHUNKS - 3
+DRAIN = CHUNKS - 2
 GP_FIRST = 4
 GP_LEAD = 2
-PAIRS_FROM = 4
-WARM_PASSES = 5
+WARM_PASSES = 2
 EPS = 1e-5
 
 FLOPS = 2 * ROWS * K * FEATURES
@@ -255,6 +254,7 @@ def tile_attention_pb_t_kernel(tc, h_attn, proj_w, proj_g, proj_b, out):
                         multiply(
                             y[:, first : first + P * CHUNK_BLOCKS[chunk]], half, cols[chunk], True, True
                         )
+                for half in range(HALVES):
                     for first in range(start, start + rows, P):
                         multiply(
                             row_sums[half][:],
@@ -362,22 +362,29 @@ def tile_attention_pb_t_kernel(tc, h_attn, proj_w, proj_g, proj_b, out):
                     transpose_weights()
 
             total = keep.tile([P, HALVES], F32)
+            off = keep.tile([P, HALVES], F32)
+            neg_off = keep.tile([P, HALVES], F32)
+            neg_mean_g = keep.tile([P, HALVES], F32)
+            sq_total = keep.tile([P, HALVES], F32)
+            sq_mean = keep.tile([P, HALVES], F32)
+            var_rest = keep.tile([P, HALVES], F32)
+            rstd = keep.tile([P, HALVES], F32)
             for half in range(HALVES):
                 nc.vector.tensor_reduce(
                     out=total[:, half : half + 1], in_=row_sums[half][:], axis=X_AXIS, op=ALU.add
                 )
-            sq_total = keep.tile([P, HALVES], F32)
             nc.vector.tensor_reduce(out=sq_total[:], in_=sq_parts[:], axis=X_AXIS, op=ALU.add)
-            neg_mean_g = keep.tile([P, HALVES], F32)
             nc.vector.scalar_tensor_tensor(
-                out=neg_mean_g[:],
-                in0=total[:],
-                scalar=-1.0 / ROWS,
-                in1=gb[:, 0:HALVES],
-                op0=ALU.mult,
-                op1=ALU.mult,
+                out=off[:], in0=total[:], scalar=-1.0 / ROWS, in1=pivot[:], op0=ALU.mult, op1=ALU.add
             )
-            sq_mean = keep.tile([P, HALVES], F32)
+            nc.vector.scalar_tensor_tensor(
+                out=neg_off[:],
+                in0=total[:],
+                scalar=1.0 / ROWS,
+                in1=pivot[:],
+                op0=ALU.mult,
+                op1=ALU.subtract,
+            )
             nc.vector.tensor_scalar(
                 out=sq_mean[:],
                 in0=sq_total[:],
@@ -386,50 +393,42 @@ def tile_attention_pb_t_kernel(tc, h_attn, proj_w, proj_g, proj_b, out):
                 op0=ALU.mult,
                 op1=ALU.add,
             )
-
-            def each_half(result, **args):
-                for half in range(HALVES):
-                    column = slice(half, half + 1)
-                    nc.scalar.activation(
-                        out=result[:, column],
-                        func=args["func"],
-                        in_=args["in_"][:, column],
-                        scale=args["scale"](column),
-                        bias=args["bias"](column),
-                    )
-
-            off_sq = keep.tile([P, HALVES], F32)
-            each_half(
-                off_sq,
-                func=ACT.Square,
-                in_=total,
-                scale=lambda c: -1.0 / ROWS,
-                bias=lambda c: pivot[:, c],
+            nc.vector.scalar_tensor_tensor(
+                out=neg_mean_g[:],
+                in0=total[:],
+                scalar=-1.0 / ROWS,
+                in1=gb[:, 0:HALVES],
+                op0=ALU.mult,
+                op1=ALU.mult,
             )
-            sq_eps = keep.tile([P, HALVES], F32)
-            each_half(
-                sq_eps,
-                func=ACT.Identity,
-                in_=sq_last,
-                scale=lambda c: 1.0 / ROWS,
-                bias=lambda c: sq_mean[:, c],
-            )
-            rstd = keep.tile([P, HALVES], F32)
-            each_half(
-                rstd,
-                func=ACT.Abs_reciprocal_sqrt,
-                in_=off_sq,
-                scale=lambda c: -1.0,
-                bias=lambda c: sq_eps[:, c],
-            )
+            for half in range(HALVES):
+                column = slice(half, half + 1)
+                nc.vector.scalar_tensor_tensor(
+                    out=var_rest[:, column],
+                    in0=off[:, column],
+                    scalar=neg_off[:, column],
+                    in1=sq_mean[:, column],
+                    op0=ALU.mult,
+                    op1=ALU.add,
+                )
+                nc.scalar.activation(
+                    out=rstd[:, column],
+                    in_=sq_last[:, column],
+                    func=ACT.Abs_reciprocal_sqrt,
+                    scale=1.0 / ROWS,
+                    bias=var_rest[:, column],
+                )
             nc.vector.tensor_tensor(out=gain[:], in0=rstd[:], in1=gb[:, 0:HALVES], op=ALU.mult)
-            each_half(
-                shift,
-                func=ACT.Identity,
-                in_=neg_mean_g,
-                scale=lambda c: rstd[:, c],
-                bias=lambda c: gb[:, slice(HALVES + c.start, HALVES + c.stop)],
-            )
+            for half in range(HALVES):
+                column = slice(half, half + 1)
+                nc.vector.scalar_tensor_tensor(
+                    out=shift[:, column],
+                    in0=rstd[:, column],
+                    scalar=neg_mean_g[:, column],
+                    in1=gb[:, HALVES + half : HALVES + half + 1],
+                    op0=ALU.mult,
+                    op1=ALU.add,
+                )
 
         with tc.psum_pool(name="psum_o", bufs=3, reuse_waits="tile") as psum_o, tc.psum_pool(
             name="psum_s", bufs=1, reuse_waits="tile"
@@ -492,7 +491,7 @@ def tile_attention_pb_t_kernel(tc, h_attn, proj_w, proj_g, proj_b, out):
                 for half in range(halves_by_features(chunk)):
                     column = slice(half, half + 1)
                     normed_half = stage.tile([P, blocks * P], F32, name="normed%d" % half, bufs=4)
-                    if half == 0:
+                    if half == 0 and chunk > 0:
                         nc.scalar.activation(
                             out=normed_half[:],
                             in_=y2_banks[(chunk, half)],
@@ -546,7 +545,7 @@ def tile_attention_pb_t_kernel(tc, h_attn, proj_w, proj_g, proj_b, out):
             def empty_and_store(chunk):
                 blocks = CHUNK_BLOCKS[chunk]
                 if chunk == 0:
-                    nc.scalar.copy(
+                    nc.vector.tensor_copy(
                         out=results[0][:].rearrange("p j (h c) -> p (j h) c", h=HALVES),
                         in_=oT_banks[(0, 0)][:],
                     )
@@ -571,34 +570,18 @@ def tile_attention_pb_t_kernel(tc, h_attn, proj_w, proj_g, proj_b, out):
             normalise(0)
             normalise(1)
             nc.vector.tensor_copy(out=rows_gs[:], in_=spread[:])
-            products_by_rows(2)
             transpose_back(0)
+            products_by_rows(2)
             transpose_back(1)
             normalise(2)
-            for chunk in range(PAIRS_FROM - 1):
-                if chunk > 1:
-                    normalise(chunk + 1)
-                if chunk > 0:
+            for chunk in range(CHUNKS):
+                if chunk > 0 and chunk + 1 < CHUNKS:
+                    if chunk > 1:
+                        normalise(chunk + 1)
                     scale_rows(chunk + 1)
                 if chunk > 1:
                     transpose_back(chunk)
-                if chunk > 0:
+                if chunk > 0 and chunk + 2 < CHUNKS:
                     products_by_features(chunk + 2)
                     products_by_rows(chunk + 2)
                 empty_and_store(chunk)
-            products_by_features(PAIRS_FROM + 1)
-            products_by_rows(PAIRS_FROM + 1)
-            for first in range(PAIRS_FROM, CHUNKS + 1, 2):
-                following = range(first + 2, min(first + 4, CHUNKS))
-                emptied = range(first - 1, min(first + 1, CHUNKS))
-                for chunk in range(first, min(first + 2, CHUNKS)):
-                    normalise(chunk)
-                    scale_rows(chunk)
-                for chunk in emptied:
-                    transpose_back(chunk)
-                for chunk in following:
-                    products_by_features(chunk)
-                for chunk in following:
-                    products_by_rows(chunk)
-                for chunk in emptied:
-                    empty_and_store(chunk)

import concourse.mybir as mybir
from concourse.masks import make_identity

FP8X4 = mybir.dt.float8_e4m3fn_x4
BF16 = mybir.dt.bfloat16
F32 = mybir.dt.float32
U32 = mybir.dt.uint32
U8 = mybir.dt.uint8
ACT = mybir.ActivationFunctionType
ALU = mybir.AluOpType
X_AXIS = mybir.AxisListType.X

P = 128
PACK = 4
WORDS = 2
SIDES = 2
SIDE = P // SIDES
K = P * PACK
ROWS = 32 * 256
FEATURES = 256
HALVES = FEATURES // P
PAIR = 2
CHUNK_BLOCKS = [1, 2] + [4] * 15 + [1]
CHUNKS = len(CHUNK_BLOCKS)
FULL = 4 * P
DRAIN = CHUNKS - 2
GP_FIRST = 4
GP_LEAD = 2
WARM_PASSES = 2
EPS = 1e-5

FLOPS = 2 * ROWS * K * FEATURES


def tile_attention_pb_t_kernel(tc, h_attn, proj_w, proj_g, proj_b, out):
    nc = tc.nc

    starts = [P * sum(CHUNK_BLOCKS[:i]) for i in range(CHUNKS)]
    cols = [slice(starts[i], starts[i] + P * CHUNK_BLOCKS[i]) for i in range(CHUNKS)]
    x_all = h_attn.flatten_outer_dims()
    out_all = out.flatten_outer_dims()
    x_chunks = [
        x_all[cols[i], :].rearrange("(p j) k -> p j k", j=CHUNK_BLOCKS[i]) for i in range(CHUNKS)
    ]
    out_chunks = [
        out_all[cols[i], :].rearrange("(p j) c -> p j c", j=CHUNK_BLOCKS[i]) for i in range(CHUNKS)
    ]
    pairs = [-(-CHUNK_BLOCKS[i] // PAIR) for i in range(CHUNKS)]

    with tc.manual_schedule(), tc.tile_pool(name="keep", bufs=1) as keep, tc.tile_pool(
        name="stage", bufs=3
    ) as stage:
        x_tiles = []

        def load(chunk):
            x_rows = keep.tile([P, CHUNK_BLOCKS[chunk], K], BF16, name="x_rows%d" % chunk)
            nc.sync.dma_start(out=x_rows[:], in_=x_chunks[chunk])
            x_tiles.append(x_rows)

        for chunk in range(3):
            load(chunk)
        w_rows = keep.tile([P, HALVES, K], BF16)
        nc.sync.dma_start(out=w_rows[:], in_=proj_w.rearrange("(h c) k -> c h k", h=HALVES))
        gb_rows = keep.tile([P, P], BF16)
        nc.vector.memset(gb_rows[:], 0.0)
        nc.sync.dma_start(
            out=gb_rows[0:HALVES, :], in_=proj_g.rearrange("(h c) -> h c", h=HALVES)
        )
        nc.sync.dma_start(
            out=gb_rows[HALVES : 2 * HALVES, :], in_=proj_b.rearrange("(h c) -> h c", h=HALVES)
        )
        for chunk in range(3, CHUNKS):
            load(chunk)

        ident_f32 = keep.tile([P, P], F32)
        make_identity(nc, ident_f32[:])
        ident_sides = keep.tile([P, SIDE, SIDES], F32)
        nc.vector.tensor_copy(
            out=ident_sides[:], in_=ident_f32[:].rearrange("i (r j) -> i j r", r=SIDES)
        )
        ident_bf16 = keep.tile([P, P], BF16)
        make_identity(nc, ident_bf16[:])

        one = keep.tile([P, 1], F32)
        nc.vector.memset(one[:], 1.0)
        nc.scalar.activation(out=one[:], in_=one[:], func=ACT.Abs_reciprocal_sqrt)

        w_codes = keep.tile([P, FEATURES], U32, align_bytes=64)
        w_scales = keep.tile([P, FEATURES], U8, align_bytes=64)
        h_codes = keep.tile([P, ROWS], U32, align_bytes=64)
        h_scales = keep.tile([P, ROWS], U8, align_bytes=64)

        def multiply(acc, half, rows, start, stop):
            features = slice(half * P, (half + 1) * P)
            nc.tensor.matmul_mx(
                out=acc,
                lhsT=w_codes[:, features].bitcast(FP8X4),
                lhsT_scale=w_scales[:, features],
                rhs=h_codes[:, rows].bitcast(FP8X4),
                rhs_scale=h_scales[:, rows],
                start=start,
                stop=stop,
            )

        gb = keep.tile([P, 2 * HALVES], F32)
        pivot = keep.tile([P, HALVES], F32)
        sq_parts = keep.tile([P, HALVES, CHUNKS - 2], F32)
        sq_last = keep.tile([P, HALVES], F32)
        gain = keep.tile([P, HALVES], F32)
        shift = keep.tile([P, HALVES], F32)

        with tc.psum_pool(name="psum_t", bufs=4) as psum_t, tc.psum_pool(
            name="psum_y", bufs=2
        ) as psum_y, tc.psum_pool(name="psum_sum", bufs=1) as psum_sum:
            row_sums = [
                psum_sum.tile([P, P], F32, name="row_sums%d" % half) for half in range(HALVES)
            ]
            xT_banks = {}
            h_rows = {}
            y_banks = {}

            def by_gpsimd(chunk, block):
                return GP_FIRST <= chunk and block == CHUNK_BLOCKS[chunk] - 1

            def pair_blocks(chunk, pair):
                return range(pair * PAIR, min((pair + 1) * PAIR, CHUNK_BLOCKS[chunk]))

            def transposes(chunk):
                for pair in range(pairs[chunk]):
                    xT = psum_t.tile([P, PAIR, SIDE, WORDS, SIDES], F32, tag="xT", name="xT")
                    for block in pair_blocks(chunk, pair):
                        if by_gpsimd(chunk, block):
                            words = h_rows[chunk][:].bitcast(F32)
                        else:
                            words = x_tiles[chunk][:, block, :].bitcast(F32)
                        for u in range(WORDS):
                            nc.tensor.transpose(
                                xT[:, block - pair * PAIR, :, u, :],
                                words[:, u : K // 2 : WORDS],
                                ident_sides[:],
                            )
                    xT_banks[(chunk, pair)] = xT

            ramp_rows = {}

            def last_block(chunk):
                return x_tiles[chunk][:, CHUNK_BLOCKS[chunk] - 1, :]

            def make_ramp_rows(chunk):
                clipped = stage.tile([P, K], BF16)
                nc.vector.tensor_scalar(
                    out=clipped[:],
                    in0=last_block(chunk),
                    scalar1=-3.0,
                    scalar2=3.0,
                    op0=ALU.max,
                    op1=ALU.min,
                )
                ramp_rows[chunk] = stage.tile([P, K], F32, name="ramp_rows")
                nc.gpsimd.tensor_scalar(
                    out=ramp_rows[chunk][:],
                    in0=clipped[:],
                    scalar1=3.0,
                    scalar2=1.0 / 6.0,
                    op0=ALU.add,
                    op1=ALU.mult,
                )

            def multiply_rows(chunk):
                h_rows[chunk] = stage.tile([P, K], BF16, name="h_block")
                nc.gpsimd.tensor_tensor(
                    out=h_rows[chunk][:],
                    in0=ramp_rows[chunk][:],
                    in1=last_block(chunk),
                    op=ALU.mult,
                )

            ramps = {}
            grouped = {}

            def side_blocks(chunk, pair):
                return len([b for b in pair_blocks(chunk, pair) if not by_gpsimd(chunk, b)])

            def by_side(chunk, pair):
                return (
                    xT_banks[(chunk, pair)][:, 0 : side_blocks(chunk, pair)]
                    .rearrange("q s j u r -> q (s j u r)")
                    .bitcast(BF16)
                    .rearrange("q (m r e) -> q r m e", r=SIDES, e=2)
                )

            def make_ramps(chunk):
                for pair in range(pairs[chunk]):
                    blocks = side_blocks(chunk, pair)
                    if blocks == 0:
                        continue
                    ramp = stage.tile([P, SIDES, blocks * SIDE * WORDS, 2], F32, name="ramp", bufs=4)
                    nc.scalar.activation(
                        out=ramp[:], in_=by_side(chunk, pair), func=ACT.Relu, scale=1.0 / 6.0, bias=0.5
                    )
                    ramps[(chunk, pair)] = ramp

            def multiply_side(chunk, pair, side):
                if pair == 0 and side == 0:
                    grouped[chunk] = stage.tile(
                        [P, CHUNK_BLOCKS[chunk], SIDES, SIDE * WORDS, 2],
                        BF16,
                        name="grouped",
                        align_bytes=64,
                    )
                blocks = side_blocks(chunk, pair)
                if blocks == 0:
                    return
                values = by_side(chunk, pair)
                nc.vector.scalar_tensor_tensor(
                    out=grouped[chunk][:, pair * PAIR : pair * PAIR + blocks, side],
                    in0=ramps[(chunk, pair)][:, side].rearrange("q (s m) e -> q s m e", s=blocks),
                    scalar=1.0,
                    in1=values[:, side].rearrange("q (s m) e -> q s m e", s=blocks),
                    op0=ALU.min,
                    op1=ALU.mult,
                )

            def take_rows(chunk):
                last = CHUNK_BLOCKS[chunk] - 1
                nc.vector.tensor_copy(
                    out=grouped[chunk][:, last]
                    .rearrange("q r m e -> q (r m e)")
                    .bitcast(F32)
                    .rearrange("q (r j u) -> q r j u", r=SIDES, u=WORDS),
                    in_=xT_banks[(chunk, last // PAIR)][:, last % PAIR].rearrange(
                        "q j u r -> q r j u"
                    ),
                )

            def quantise(chunk):
                nc.vector.quantize_mx(
                    out=h_codes[:, cols[chunk]].bitcast(FP8X4),
                    scales=h_scales[:, cols[chunk]],
                    in_=grouped[chunk][:].rearrange("q b r m e -> q (b r m e)"),
                )

            def products(*chunks):
                start = starts[chunks[0]]
                rows = P * sum(CHUNK_BLOCKS[chunk] for chunk in chunks)
                for half in range(HALVES):
                    if chunks[0] < DRAIN:
                        y = psum_y.tile([P, rows], F32, tag="y", name="y")
                    else:
                        y = psum_t.tile([P, rows], F32, tag="xT", name="y")
                    y_banks[(chunks[0], half)] = y
                    for chunk in chunks:
                        first = starts[chunk] - start
                        multiply(
                            y[:, first : first + P * CHUNK_BLOCKS[chunk]], half, cols[chunk], True, True
                        )
                for half in range(HALVES):
                    for first in range(start, start + rows, P):
                        multiply(
                            row_sums[half][:],
                            half,
                            slice(first, first + P),
                            first == 0,
                            first == ROWS - P,
                        )

            def choose_pivot():
                for half in range(HALVES):
                    unread = stage.tile([P, FULL], BF16, name="unread")
                    nc.scalar.activation(
                        out=unread[:, 0:P],
                        in_=y_banks[(0, half)][:, 0:P],
                        func=ACT.Identity,
                        scale=1.0 / P,
                        accum_out=pivot[:, half : half + 1],
                    )

            def squares(chunk):
                for half in range(HALVES):
                    y = y_banks[(chunk, half)]
                    unread = stage.tile([P, FULL], BF16, name="unread")
                    if chunk < CHUNKS - 1:
                        column = max(chunk - 1, 0)
                        sum_of_squares = sq_parts[:, half, column : column + 1]
                    else:
                        sum_of_squares = sq_last[:, half : half + 1]
                    nc.scalar.activation(
                        out=unread[:, 0 : y.shape[1]],
                        in_=y[:],
                        func=ACT.Square,
                        scale=-1.0,
                        bias=pivot[:, half : half + 1],
                        accum_out=sum_of_squares,
                    )

            wT = psum_y.tile([P, WORDS, FEATURES], F32, tag="y", name="wT")
            gbT = psum_y.tile([P, P], BF16, tag="y", name="gbT")
            w_grouped = keep.tile([P, FEATURES * PACK], BF16, align_bytes=64)

            def transpose_weights():
                for half in range(HALVES):
                    words = w_rows[:, half, :].bitcast(F32)
                    for u in range(WORDS):
                        nc.tensor.transpose(
                            wT[:, u, half * P : (half + 1) * P],
                            words[:, u : K // 2 : WORDS],
                            ident_f32[:],
                        )
                nc.tensor.transpose(gbT[:], gb_rows[:], ident_bf16[:])

            def group_weights():
                nc.scalar.copy(
                    out=w_grouped[:].bitcast(F32).rearrange("q (c u) -> q c u", u=WORDS),
                    in_=wT[:].rearrange("q u c -> q c u"),
                )
                nc.scalar.copy(out=gb[:], in_=gbT[:, 0 : 2 * HALVES])

            def quantise_weights():
                nc.vector.quantize_mx(
                    out=w_codes[:].bitcast(FP8X4), scales=w_scales[:], in_=w_grouped[:]
                )

            transposes(0)
            transposes(1)
            for step in range(CHUNKS + 2):
                if step < CHUNKS:
                    make_ramps(step)
                    multiply_side(step, 0, 0)
                if step == CHUNKS - 1:
                    take_rows(step)
                if step == 2:
                    group_weights()
                if 1 <= step <= CHUNKS:
                    if GP_FIRST < step + GP_LEAD + 1 < CHUNKS:
                        make_ramp_rows(step + GP_LEAD + 1)
                    if GP_FIRST <= step + GP_LEAD < CHUNKS:
                        multiply_rows(step + GP_LEAD)
                    quantise(step - 1)
                if step < CHUNKS:
                    multiply_side(step, 0, 1)
                if step == 2:
                    quantise_weights()
                    products(0, 1)
                if 2 < step <= CHUNKS:
                    products(step - 1)
                if step < CHUNKS:
                    if pairs[step] > 1:
                        multiply_side(step, 1, 0)
                        multiply_side(step, 1, 1)
                    if GP_FIRST <= step < CHUNKS - 1:
                        take_rows(step)
                if step + GP_LEAD + 1 == GP_FIRST:
                    make_ramp_rows(GP_FIRST)
                if step == 3:
                    choose_pivot()
                    squares(0)
                if step > 3:
                    squares(step - 2)
                if step + 2 < CHUNKS:
                    transposes(step + 2)
                if step == 0:
                    transpose_weights()

            total = keep.tile([P, HALVES], F32)
            off = keep.tile([P, HALVES], F32)
            neg_off = keep.tile([P, HALVES], F32)
            neg_mean_g = keep.tile([P, HALVES], F32)
            sq_total = keep.tile([P, HALVES], F32)
            sq_mean = keep.tile([P, HALVES], F32)
            var_rest = keep.tile([P, HALVES], F32)
            rstd = keep.tile([P, HALVES], F32)
            for half in range(HALVES):
                nc.vector.tensor_reduce(
                    out=total[:, half : half + 1], in_=row_sums[half][:], axis=X_AXIS, op=ALU.add
                )
            nc.vector.tensor_reduce(out=sq_total[:], in_=sq_parts[:], axis=X_AXIS, op=ALU.add)
            nc.vector.scalar_tensor_tensor(
                out=off[:], in0=total[:], scalar=-1.0 / ROWS, in1=pivot[:], op0=ALU.mult, op1=ALU.add
            )
            nc.vector.scalar_tensor_tensor(
                out=neg_off[:],
                in0=total[:],
                scalar=1.0 / ROWS,
                in1=pivot[:],
                op0=ALU.mult,
                op1=ALU.subtract,
            )
            nc.vector.tensor_scalar(
                out=sq_mean[:],
                in0=sq_total[:],
                scalar1=1.0 / ROWS,
                scalar2=EPS,
                op0=ALU.mult,
                op1=ALU.add,
            )
            nc.vector.scalar_tensor_tensor(
                out=neg_mean_g[:],
                in0=total[:],
                scalar=-1.0 / ROWS,
                in1=gb[:, 0:HALVES],
                op0=ALU.mult,
                op1=ALU.mult,
            )
            for half in range(HALVES):
                column = slice(half, half + 1)
                nc.vector.scalar_tensor_tensor(
                    out=var_rest[:, column],
                    in0=off[:, column],
                    scalar=neg_off[:, column],
                    in1=sq_mean[:, column],
                    op0=ALU.mult,
                    op1=ALU.add,
                )
                nc.scalar.activation(
                    out=rstd[:, column],
                    in_=sq_last[:, column],
                    func=ACT.Abs_reciprocal_sqrt,
                    scale=1.0 / ROWS,
                    bias=var_rest[:, column],
                )
            nc.vector.tensor_tensor(out=gain[:], in0=rstd[:], in1=gb[:, 0:HALVES], op=ALU.mult)
            for half in range(HALVES):
                column = slice(half, half + 1)
                nc.vector.scalar_tensor_tensor(
                    out=shift[:, column],
                    in0=rstd[:, column],
                    scalar=neg_mean_g[:, column],
                    in1=gb[:, HALVES + half : HALVES + half + 1],
                    op0=ALU.mult,
                    op1=ALU.add,
                )

        with tc.psum_pool(name="psum_o", bufs=3, reuse_waits="tile") as psum_o, tc.psum_pool(
            name="psum_s", bufs=1, reuse_waits="tile"
        ) as psum_s, tc.psum_pool(name="psum_y2", bufs=2, reuse_waits="tile") as psum_y2, tc.psum_pool(
            name="psum_r", bufs=2, reuse_waits="tile"
        ) as psum_r:
            y2_banks = {}
            yR_banks = {}
            normed = {}
            scaled_rows = {}
            oT_banks = {}
            results = {}
            rows_gs = keep.tile([P, 2, P], F32)
            last_half = HALVES - 1
            last_features = slice(last_half * P, HALVES * P)

            def halves_by_features(chunk):
                return HALVES if chunk < 2 else 1

            def products_by_features(chunk):
                rows = P * CHUNK_BLOCKS[chunk]
                if chunk == 1:
                    banks = [psum_r.tile([P, rows], F32, tag="yR", name="y2") for half in range(HALVES)]
                    parts = [bank[:] for bank in banks]
                else:
                    bank = psum_y2.tile([P, halves_by_features(chunk), rows], F32, tag="y2", name="y2")
                    parts = [bank[:, half, :] for half in range(halves_by_features(chunk))]
                for half in range(len(parts)):
                    multiply(parts[half], half, cols[chunk], True, True)
                    y2_banks[(chunk, half)] = parts[half]

            def products_by_rows(chunk):
                yR = psum_r.tile([P, CHUNK_BLOCKS[chunk], P], F32, tag="yR", name="yR")
                for block in range(CHUNK_BLOCKS[chunk]):
                    rows = slice(starts[chunk] + block * P, starts[chunk] + (block + 1) * P)
                    nc.tensor.matmul_mx(
                        out=yR[:, block, :],
                        lhsT=h_codes[:, rows].bitcast(FP8X4),
                        lhsT_scale=h_scales[:, rows],
                        rhs=w_codes[:, last_features].bitcast(FP8X4),
                        rhs_scale=w_scales[:, last_features],
                        start=True,
                        stop=True,
                    )
                yR_banks[chunk] = yR

            def spread_gain_and_shift():
                spread = psum_s.tile([P, 2, P], F32, name="spread")
                for which, numbers in enumerate((gain, shift)):
                    nc.tensor.transpose(
                        spread[:, which, :],
                        numbers[:, last_half:HALVES].to_broadcast([P, P]),
                        ident_f32[:],
                    )
                return spread

            def normalise(chunk):
                blocks = CHUNK_BLOCKS[chunk]
                results[chunk] = stage.tile([P, blocks, FEATURES], F32, name="result", bufs=10)
                for half in range(halves_by_features(chunk)):
                    column = slice(half, half + 1)
                    normed_half = stage.tile([P, blocks * P], F32, name="normed%d" % half, bufs=4)
                    if half == 0 and chunk > 0:
                        nc.scalar.activation(
                            out=normed_half[:],
                            in_=y2_banks[(chunk, half)],
                            func=ACT.Identity,
                            scale=gain[:, column],
                            bias=shift[:, column],
                        )
                    else:
                        nc.vector.tensor_scalar(
                            out=normed_half[:],
                            in0=y2_banks[(chunk, half)],
                            scalar1=gain[:, column],
                            scalar2=shift[:, column],
                            op0=ALU.mult,
                            op1=ALU.add,
                        )
                    normed[(chunk, half)] = normed_half

            def scale_rows(chunk):
                blocks = CHUNK_BLOCKS[chunk]
                scaled_rows[chunk] = stage.tile([P, blocks, P], F32, name="scaled", bufs=4)
                nc.vector.tensor_tensor(
                    out=scaled_rows[chunk][:],
                    in0=yR_banks[chunk][:],
                    in1=rows_gs[:, 0:1, :].to_broadcast([P, blocks, P]),
                    op=ALU.mult,
                )

            def shift_rows(chunk):
                engine, shifts = (nc.vector, spread) if chunk % 3 == 1 else (nc.gpsimd, rows_gs)
                engine.tensor_tensor(
                    out=results[chunk][:, :, last_features],
                    in0=scaled_rows[chunk][:],
                    in1=shifts[:, 1:2, :].to_broadcast([P, CHUNK_BLOCKS[chunk], P]),
                    op=ALU.add,
                )

            def transpose_back(chunk):
                blocks = CHUNK_BLOCKS[chunk]
                for half in range(halves_by_features(chunk)):
                    if chunk > 0 or half == 0:
                        oT = psum_o.tile([P, max(blocks, HALVES), P], F32, tag="oT", name="oT")
                    for block in range(blocks):
                        nc.tensor.transpose(
                            oT[:, half if chunk == 0 else block, :],
                            normed[(chunk, half)][:, block * P : (block + 1) * P],
                            ident_f32[:],
                        )
                    oT_banks[(chunk, half)] = oT

            def empty_and_store(chunk):
                blocks = CHUNK_BLOCKS[chunk]
                if chunk == 0:
                    nc.vector.tensor_copy(
                        out=results[0][:].rearrange("p j (h c) -> p (j h) c", h=HALVES),
                        in_=oT_banks[(0, 0)][:],
                    )
                else:
                    for half in range(halves_by_features(chunk)):
                        by_vector = half == last_half or (chunk > 2 and chunk % 3 == 2)
                        copy = nc.vector.tensor_copy if by_vector else nc.scalar.copy
                        copy(
                            out=results[chunk][:, :, half * P : (half + 1) * P],
                            in_=oT_banks[(chunk, half)][:, 0:blocks, :],
                        )
                if chunk + 1 < CHUNKS and chunk > 0:
                    shift_rows(chunk + 1)
                nc.sync.dma_start(out=out_chunks[chunk], in_=results[chunk][:])

            products_by_features(0)
            products_by_features(1)
            products_by_features(2)
            for again in range(WARM_PASSES):
                multiply(y2_banks[(2, 0)], 0, cols[2], True, True)
            spread = spread_gain_and_shift()
            normalise(0)
            normalise(1)
            nc.vector.tensor_copy(out=rows_gs[:], in_=spread[:])
            transpose_back(0)
            products_by_rows(2)
            transpose_back(1)
            normalise(2)
            for chunk in range(CHUNKS):
                if chunk > 0 and chunk + 1 < CHUNKS:
                    if chunk > 1:
                        normalise(chunk + 1)
                    scale_rows(chunk + 1)
                if chunk > 1:
                    transpose_back(chunk)
                if chunk > 0 and chunk + 2 < CHUNKS:
                    products_by_features(chunk + 2)
                    products_by_rows(chunk + 2)
                empty_and_store(chunk)
